import numpy as np
import ml_dtypes


def mxq(x, axis, fmt="e4m3"):
    dtype, down = {"e4m3": (ml_dtypes.float8_e4m3fn, 7), "e5m2": (ml_dtypes.float8_e5m2, 14)}[fmt]
    v = np.moveaxis(np.asarray(x, np.float32).astype(ml_dtypes.bfloat16).astype(np.float64), axis, -1)
    blocks = v.reshape(v.shape[:-1] + (-1, 32))
    amax = np.abs(blocks).max(-1, keepdims=True)
    byte = np.maximum(np.where(amax > 0, np.frexp(amax)[1] - 1 + 127, 0) - down, 1)
    scale = np.exp2(byte - 127.0)
    codes = (blocks / scale).astype(np.float32).astype(dtype).astype(np.float64)
    return np.moveaxis((codes * scale).reshape(v.shape), -1, axis)


WIDE = False


def mx_kscale(k):
    if not WIDE:
        return np.ones(k)
    levels = np.array([20, -20, 10, -10, 0])
    a = np.random.permutation(np.resize(levels, k // 512 * 4)).reshape(k // 512, 4)
    idx = np.arange(k)
    return np.exp2(a[idx // 512, idx % 128 // 32])


BF16 = ml_dtypes.bfloat16


def bf(x):
    return np.asarray(x, np.float32).astype(BF16)


def f64(x):
    return np.asarray(x).astype(np.float64)


B, IN, H, G, GA, GB = 1024, 1024, 1024, 6, 4, 2
EPS = 1e-5


def layer_norm(v, g, b):
    mu = v.mean(-1, keepdims=True)
    var = np.square(v - mu).mean(-1, keepdims=True)
    return (v - mu) / np.sqrt(var + EPS) * g + b


def sigmoid(v):
    return 1.0 / (1.0 + np.exp(-v))


def gate_parts(x, h, W_u, U_u, ln_gamma, ln_beta):
    g_uh, g_ux = ln_gamma
    b_uh, b_ux = ln_beta
    v = x @ U_u.T
    mu = v.mean(-1, keepdims=True)
    var = np.square(v - mu).mean(-1, keepdims=True)
    rstd = 1.0 / np.sqrt(var + EPS)
    xn = (v - mu) * rstd
    u = sigmoid(layer_norm(h @ W_u.T, g_uh, b_uh) + xn * g_ux + b_ux)
    return u, xn, rstd


def setup_inputs():
    s = mx_kscale(B)[:, None]
    x0 = bf(np.random.standard_normal((B, IN)))
    h = bf(np.random.standard_normal((B, H)))
    c = bf(np.tanh(1.4 * np.random.standard_normal((B, H))))
    W_u = bf(np.random.standard_normal((H, H)) / np.sqrt(H))
    U_u = bf(np.random.standard_normal((H, IN)) / np.sqrt(IN))
    ln_gamma = bf(1.0 + 0.1 * np.random.standard_normal((GB, H)))
    ln_beta = bf(0.2 * np.random.standard_normal((GB, H)))
    g = bf(np.random.standard_normal((B, H)) * np.exp2(np.random.randint(-12, 1, (B, 1))) / s)
    u, xn, rstd = gate_parts(f64(x0), f64(h), f64(W_u), f64(U_u), f64(ln_gamma), f64(ln_beta))
    return {"x": bf(f64(x0) * s), "h": h, "c": c, "W_u": W_u, "U_u": U_u,
            "ln_gamma": ln_gamma, "ln_beta": ln_beta,
            "u": np.asarray(u, np.float32), "xn": np.asarray(xn, np.float32), "rstd": np.asarray(rstd, np.float32),
            "grad_out": g}


def reference(x, h, c, W_u, U_u, ln_gamma, ln_beta, u, xn, rstd, grad_out):
    uf = f64(u)
    xh = f64(xn)
    da = f64(grad_out) * (f64(c) - f64(h)) * uf * (1.0 - uf)
    dn = da * f64(ln_gamma)[1]
    dv = f64(rstd) * (dn - dn.mean(-1, keepdims=True) - xh * (dn * xh).mean(-1, keepdims=True))
    return mxq(dv, 0, "e5m2").T @ mxq(f64(x), 0, "e4m3")

@@ -1,0 +1,196 @@
+import concourse.mybir as mybir
+
+F32 = mybir.dt.float32
+BF16 = mybir.dt.bfloat16
+I32 = mybir.dt.int32
+U32 = mybir.dt.uint32
+U8 = mybir.dt.uint8
+E4M3_X4 = mybir.dt.float8_e4m3fn_x4
+E5M2_X4 = mybir.dt.float8_e5m2_x4
+ALU = mybir.AluOpType
+ACT = mybir.ActivationFunctionType
+
+P = 128
+PACK = 4
+ROWS = 1024
+COLS = 1024
+PASSES = ROWS // (P * PACK)
+GROUPS = PASSES * PACK
+M_TILE = 128
+N_TILE = 512
+BLOCKS = COLS // M_TILE
+HALVES = COLS // N_TILE
+RUN = 4
+
+FLOPS = 2 * ROWS * COLS * COLS
+BYTES = 4 * ROWS * COLS * 2 + 2 * ROWS * COLS * 4 + COLS * COLS * 4 + COLS * 2 + ROWS * 4
+
+
+def by_group(matrix):
+    return matrix.rearrange("(c p j) w -> p c j w", c=PASSES, p=P, j=PACK)
+
+
+def regroup(nc, grouped, rows):
+    nc.scalar.copy(
+        out=grouped.rearrange("p (q i) j -> p q j i", i=RUN),
+        in_=rows.rearrange("p j (q i) -> p q j i", i=RUN),
+    )
+
+
+def tile_layernormgrucell_pb_v_kernel(
+    tc, x, h, c, W_u, U_u, ln_gamma, ln_beta, u, xn, rstd, grad_out, out
+):
+    nc = tc.nc
+    with (
+        tc.manual_schedule(),
+        tc.tile_pool(name="resident", bufs=1) as resident,
+        tc.tile_pool(name="scratch", bufs=4) as scratch,
+        tc.tile_pool(name="block", bufs=3) as block,
+        tc.tile_pool(name="result", bufs=6) as result,
+        tc.psum_pool(name="spread", bufs=1) as spread,
+        tc.psum_pool(name="banks", bufs=6) as banks,
+    ):
+        u_sb = resident.tile([P, GROUPS, COLS], F32)
+        xn_sb = resident.tile([P, GROUPS, COLS], F32)
+        h_sb = resident.tile([P, GROUPS, COLS], BF16)
+        c_sb = resident.tile([P, GROUPS, COLS], BF16)
+        g_sb = resident.tile([P, GROUPS, COLS], BF16)
+        x_sb = resident.tile([P, GROUPS, COLS], BF16)
+        x_grouped = resident.tile([P, PASSES, COLS, PACK], BF16, align_bytes=64)
+        x_codes = resident.tile([P, PASSES, COLS], U32, align_bytes=64)
+        x_scales = resident.tile([P, PASSES, COLS], U8, align_bytes=64)
+        rstd_sb = resident.tile([P, GROUPS], F32)
+        sum_dn = resident.tile([P, GROUPS], F32)
+        sum_dn_xn = resident.tile([P, GROUPS], F32)
+        gamma_row = resident.tile([P, COLS], BF16)
+        ones = resident.tile([P, P], BF16)
+        gamma_sb = resident.tile([P, COLS], BF16)
+
+        def load(tile_sb, matrix, g):
+            nc.sync.dma_start(out=tile_sb[:, g, :], in_=by_group(matrix)[:, g // PACK, g % PACK, :])
+
+        def load_pair(first):
+            for tile_sb, matrix in ((u_sb, u), (h_sb, h), (c_sb, c), (g_sb, grad_out), (xn_sb, xn)):
+                for g in (first, first + 1):
+                    load(tile_sb, matrix, g)
+
+        load_pair(0)
+        load_pair(2)
+        for g in range(GROUPS):
+            load(x_sb, x, g)
+        load_pair(4)
+        load_pair(6)
+
+        nc.vector.memset(gamma_row[:].bitcast(I32), 0)
+        nc.vector.memset(ones[:], 1.0)
+        nc.scalar.dma_start(out=gamma_row[0:1, :], in_=ln_gamma[1:2, :])
+        nc.scalar.dma_start(
+            out=rstd_sb[:].rearrange("p (c j) -> p c j", j=PACK),
+            in_=rstd.rearrange("(c p j) o -> p c (j o)", c=PASSES, p=P, j=PACK),
+        )
+        gamma_ps = spread.tile([P, COLS], BF16)
+        for n in range(HALVES):
+            cols = slice(n * N_TILE, (n + 1) * N_TILE)
+            nc.tensor.matmul(out=gamma_ps[:, cols], lhsT=ones[:], rhs=gamma_row[:, cols], start=True, stop=True)
+        nc.scalar.copy(out=gamma_sb[:], in_=gamma_ps[:])
+
+        def chain(pair):
+            diff = {}
+            for g in pair:
+                nc.vector.scalar_tensor_tensor(
+                    out=u_sb[:, g, :], in0=u_sb[:, g, :], scalar=1.0, in1=u_sb[:, g, :],
+                    op0=ALU.subtract, op1=ALU.mult,
+                )
+            for g in pair:
+                diff[g] = scratch.tile([P, COLS], F32, name="diff")
+                nc.vector.tensor_tensor(out=diff[g][:], in0=h_sb[:, g, :], in1=c_sb[:, g, :], op=ALU.subtract)
+            for g in pair:
+                nc.vector.tensor_tensor(out=u_sb[:, g, :], in0=u_sb[:, g, :], in1=diff[g][:], op=ALU.mult)
+            for g in pair:
+                nc.vector.tensor_tensor(out=u_sb[:, g, :], in0=u_sb[:, g, :], in1=g_sb[:, g, :], op=ALU.mult)
+            for g in pair:
+                nc.vector.scalar_tensor_tensor(
+                    out=u_sb[:, g, :], in0=u_sb[:, g, :], scalar=rstd_sb[:, g : g + 1], in1=gamma_sb[:],
+                    op0=ALU.mult, op1=ALU.mult, accum_out=sum_dn[:, g : g + 1],
+                )
+            for g in pair:
+                nc.vector.scalar_tensor_tensor(
+                    out=diff[g][:], in0=u_sb[:, g, :], scalar=1.0, in1=xn_sb[:, g, :],
+                    op0=ALU.mult, op1=ALU.mult, accum_out=sum_dn_xn[:, g : g + 1],
+                )
+            for g in pair:
+                nc.scalar.activation(
+                    out=xn_sb[:, g, :], in_=xn_sb[:, g, :], func=ACT.Identity,
+                    scale=sum_dn_xn[:, g : g + 1], bias=sum_dn[:, g : g + 1],
+                )
+
+        chain((0, 1))
+        for cc in range(PASSES):
+            for n in range(HALVES):
+                cols = slice(n * N_TILE, (n + 1) * N_TILE)
+                regroup(nc, x_grouped[:, cc, cols, :], x_sb[:, cc * PACK : (cc + 1) * PACK, cols])
+        chain((2, 3))
+        chain((4, 5))
+        chain((6, 7))
+        for cc in range(PASSES):
+            nc.vector.quantize_mx(
+                out=x_codes[:, cc, :].bitcast(E4M3_X4),
+                scales=x_scales[:, cc, :],
+                in_=x_grouped[:, cc, :, :].rearrange("p w j -> p (w j)"),
+            )
+
+        dv_rows, dv_grouped, dv_codes, dv_scales, acc = {}, {}, {}, {}, {}
+
+        def finish_dv(m):
+            cols = slice(m * M_TILE, (m + 1) * M_TILE)
+            dv_rows[m] = block.tile([P, GROUPS, M_TILE], BF16, name="dv_rows")
+            nc.vector.scalar_tensor_tensor(
+                out=dv_rows[m][:], in0=xn_sb[:, :, cols], scalar=-1.0 / COLS, in1=u_sb[:, :, cols],
+                op0=ALU.mult, op1=ALU.add,
+            )
+            dv_grouped[m] = block.tile([P, PASSES, M_TILE, PACK], BF16, name="dv_grouped", align_bytes=64)
+            for cc in range(PASSES):
+                regroup(nc, dv_grouped[m][:, cc, :, :], dv_rows[m][:, cc * PACK : (cc + 1) * PACK, :])
+
+        def quantise_dv(m):
+            dv_codes[m] = block.tile([P, PASSES, M_TILE], U32, name="dv_codes", align_bytes=64)
+            dv_scales[m] = block.tile([P, PASSES, M_TILE], U8, name="dv_scales", align_bytes=64)
+            nc.vector.quantize_mx(
+                out=dv_codes[m][:].rearrange("p c w -> p (c w)").bitcast(E5M2_X4),
+                scales=dv_scales[m][:].rearrange("p c w -> p (c w)"),
+                in_=dv_grouped[m][:].rearrange("p c w j -> p (c w j)"),
+            )
+
+        def multiply(m):
+            for n in range(HALVES):
+                cols = slice(n * N_TILE, (n + 1) * N_TILE)
+                acc[m, n] = banks.tile([P, N_TILE], F32, name="acc")
+                for cc in range(PASSES):
+                    nc.tensor.matmul_mx(
+                        out=acc[m, n][:],
+                        lhsT=dv_codes[m][:, cc, :].bitcast(E5M2_X4),
+                        lhsT_scale=dv_scales[m][:, cc, :],
+                        rhs=x_codes[:, cc, cols].bitcast(E4M3_X4),
+                        rhs_scale=x_scales[:, cc, cols],
+                        start=(cc == 0),
+                        stop=(cc == PASSES - 1),
+                    )
+
+        def store(m):
+            for n, copy in ((0, nc.vector.tensor_copy), (1, nc.scalar.copy)):
+                out_sb = result.tile([P, N_TILE], F32, name="out_sb")
+                copy(out=out_sb[:], in_=acc[m, n][:])
+                nc.sync.dma_start(
+                    out=out[m * M_TILE : (m + 1) * M_TILE, n * N_TILE : (n + 1) * N_TILE], in_=out_sb[:]
+                )
+
+        finish_dv(0)
+        finish_dv(1)
+        for m in range(BLOCKS):
+            if m + 2 < BLOCKS:
+                finish_dv(m + 2)
+            quantise_dv(m)
+            multiply(m)
+            if m > 0:
+                store(m - 1)
+        store(BLOCKS - 1)

@@ -61,7 +61,8 @@ def tile_layernormgrucell_pb_v_kernel(
         x_scales = resident.tile([P, PASSES, COLS], U8, align_bytes=64)
         rstd_sb = resident.tile([P, GROUPS], F32)
         sum_dn = resident.tile([P, GROUPS], F32)
-        sum_dn_xn = resident.tile([P, GROUPS], F32)
+        mean_dn = resident.tile([P, GROUPS], F32)
+        mean_dn_xn = resident.tile([P, GROUPS], F32)
         gamma_row = resident.tile([P, COLS], BF16)
         ones = resident.tile([P, P], BF16)
         gamma_sb = resident.tile([P, COLS], BF16)
@@ -115,13 +116,15 @@ def tile_layernormgrucell_pb_v_kernel(
                 )
             for g in pair:
                 nc.vector.scalar_tensor_tensor(
-                    out=diff[g][:], in0=u_sb[:, g, :], scalar=1.0, in1=xn_sb[:, g, :],
-                    op0=ALU.mult, op1=ALU.mult, accum_out=sum_dn_xn[:, g : g + 1],
+                    out=diff[g][:], in0=u_sb[:, g, :], scalar=1.0 / COLS, in1=xn_sb[:, g, :],
+                    op0=ALU.mult, op1=ALU.mult, accum_out=mean_dn_xn[:, g : g + 1],
                 )
+            for g in pair:
+                nc.scalar.mul(out=mean_dn[:, g : g + 1], in_=sum_dn[:, g : g + 1], mul=1.0 / COLS)
             for g in pair:
                 nc.scalar.activation(
                     out=xn_sb[:, g, :], in_=xn_sb[:, g, :], func=ACT.Identity,
-                    scale=sum_dn_xn[:, g : g + 1], bias=sum_dn[:, g : g + 1],
+                    scale=mean_dn_xn[:, g : g + 1], bias=mean_dn[:, g : g + 1],
                 )
 
         chain((0, 1))
@@ -139,18 +142,19 @@ def tile_layernormgrucell_pb_v_kernel(
                 in_=x_grouped[:, cc, :, :].rearrange("p w j -> p (w j)"),
             )
 
-        dv_rows, dv_grouped, dv_codes, dv_scales, acc = {}, {}, {}, {}, {}
+        dv_grouped, dv_codes, dv_scales, acc = {}, {}, {}, {}
 
         def finish_dv(m):
             cols = slice(m * M_TILE, (m + 1) * M_TILE)
-            dv_rows[m] = block.tile([P, GROUPS, M_TILE], BF16, name="dv_rows")
-            nc.vector.scalar_tensor_tensor(
-                out=dv_rows[m][:], in0=xn_sb[:, :, cols], scalar=-1.0 / COLS, in1=u_sb[:, :, cols],
-                op0=ALU.mult, op1=ALU.add,
-            )
             dv_grouped[m] = block.tile([P, PASSES, M_TILE, PACK], BF16, name="dv_grouped", align_bytes=64)
             for cc in range(PASSES):
-                regroup(nc, dv_grouped[m][:, cc, :, :], dv_rows[m][:, cc * PACK : (cc + 1) * PACK, :])
+                groups = slice(cc * PACK, (cc + 1) * PACK)
+                nc.vector.tensor_tensor(
+                    out=dv_grouped[m][:, cc, :, :].rearrange("p (q i) j -> p q j i", i=RUN),
+                    in0=u_sb[:, groups, cols].rearrange("p j (q i) -> p q j i", i=RUN),
+                    in1=xn_sb[:, groups, cols].rearrange("p j (q i) -> p q j i", i=RUN),
+                    op=ALU.subtract,
+                )
 
         def quantise_dv(m):
             dv_codes[m] = block.tile([P, PASSES, M_TILE], U32, name="dv_codes", align_bytes=64)
@@ -177,20 +181,17 @@ def tile_layernormgrucell_pb_v_kernel(
                     )
 
         def store(m):
-            for n, copy in ((0, nc.vector.tensor_copy), (1, nc.scalar.copy)):
+            for n in range(HALVES):
                 out_sb = result.tile([P, N_TILE], F32, name="out_sb")
-                copy(out=out_sb[:], in_=acc[m, n][:])
+                nc.scalar.copy(out=out_sb[:], in_=acc[m, n][:])
                 nc.sync.dma_start(
                     out=out[m * M_TILE : (m + 1) * M_TILE, n * N_TILE : (n + 1) * N_TILE], in_=out_sb[:]
                 )
 
         finish_dv(0)
-        finish_dv(1)
         for m in range(BLOCKS):
-            if m + 2 < BLOCKS:
-                finish_dv(m + 2)
+            if m + 1 < BLOCKS:
+                finish_dv(m + 1)
             quantise_dv(m)
             multiply(m)
-            if m > 0:
-                store(m - 1)
-        store(BLOCKS - 1)
+            store(m)

@@ -71,8 +71,12 @@ def tile_layernormgrucell_pb_v_kernel(
             nc.sync.dma_start(out=tile_sb[:, g, :], in_=by_group(matrix)[:, g // PACK, g % PACK, :])
 
         def load_pair(first):
-            for tile_sb, matrix in ((u_sb, u), (h_sb, h), (c_sb, c), (g_sb, grad_out), (xn_sb, xn)):
-                for g in (first, first + 1):
+            pair = (first, first + 1)
+            for g in pair:
+                load(h_sb, h, g)
+                load(c_sb, c, g)
+            for tile_sb, matrix in ((u_sb, u), (g_sb, grad_out), (xn_sb, xn)):
+                for g in pair:
                     load(tile_sb, matrix, g)
 
         load_pair(0)
@@ -98,13 +102,13 @@ def tile_layernormgrucell_pb_v_kernel(
         def chain(pair):
             diff = {}
             for g in pair:
+                diff[g] = scratch.tile([P, COLS], F32, name="diff")
+                nc.vector.tensor_tensor(out=diff[g][:], in0=h_sb[:, g, :], in1=c_sb[:, g, :], op=ALU.subtract)
+            for g in pair:
                 nc.vector.scalar_tensor_tensor(
                     out=u_sb[:, g, :], in0=u_sb[:, g, :], scalar=1.0, in1=u_sb[:, g, :],
                     op0=ALU.subtract, op1=ALU.mult,
                 )
-            for g in pair:
-                diff[g] = scratch.tile([P, COLS], F32, name="diff")
-                nc.vector.tensor_tensor(out=diff[g][:], in0=h_sb[:, g, :], in1=c_sb[:, g, :], op=ALU.subtract)
             for g in pair:
                 nc.vector.tensor_tensor(out=u_sb[:, g, :], in0=u_sb[:, g, :], in1=diff[g][:], op=ALU.mult)
             for g in pair:
@@ -156,29 +160,30 @@ def tile_layernormgrucell_pb_v_kernel(
                     op=ALU.subtract,
                 )
 
-        def quantise_dv(m):
-            dv_codes[m] = block.tile([P, PASSES, M_TILE], U32, name="dv_codes", align_bytes=64)
-            dv_scales[m] = block.tile([P, PASSES, M_TILE], U8, name="dv_scales", align_bytes=64)
+        def quantise_dv(m, cc):
+            if cc == 0:
+                dv_codes[m] = block.tile([P, PASSES, M_TILE], U32, name="dv_codes", align_bytes=64)
+                dv_scales[m] = block.tile([P, PASSES, M_TILE], U8, name="dv_scales", align_bytes=64)
             nc.vector.quantize_mx(
-                out=dv_codes[m][:].rearrange("p c w -> p (c w)").bitcast(E5M2_X4),
-                scales=dv_scales[m][:].rearrange("p c w -> p (c w)"),
-                in_=dv_grouped[m][:].rearrange("p c w j -> p (c w j)"),
+                out=dv_codes[m][:, cc, :].bitcast(E5M2_X4),
+                scales=dv_scales[m][:, cc, :],
+                in_=dv_grouped[m][:, cc, :, :].rearrange("p w j -> p (w j)"),
             )
 
-        def multiply(m):
+        def multiply(m, cc):
             for n in range(HALVES):
                 cols = slice(n * N_TILE, (n + 1) * N_TILE)
-                acc[m, n] = banks.tile([P, N_TILE], F32, name="acc")
-                for cc in range(PASSES):
-                    nc.tensor.matmul_mx(
-                        out=acc[m, n][:],
-                        lhsT=dv_codes[m][:, cc, :].bitcast(E5M2_X4),
-                        lhsT_scale=dv_scales[m][:, cc, :],
-                        rhs=x_codes[:, cc, cols].bitcast(E4M3_X4),
-                        rhs_scale=x_scales[:, cc, cols],
-                        start=(cc == 0),
-                        stop=(cc == PASSES - 1),
-                    )
+                if cc == 0:
+                    acc[m, n] = banks.tile([P, N_TILE], F32, name="acc")
+                nc.tensor.matmul_mx(
+                    out=acc[m, n][:],
+                    lhsT=dv_codes[m][:, cc, :].bitcast(E5M2_X4),
+                    lhsT_scale=dv_scales[m][:, cc, :],
+                    rhs=x_codes[:, cc, cols].bitcast(E4M3_X4),
+                    rhs_scale=x_scales[:, cc, cols],
+                    start=(cc == 0),
+                    stop=(cc == PASSES - 1),
+                )
 
         def store(m):
             for n in range(HALVES):
@@ -192,6 +197,7 @@ def tile_layernormgrucell_pb_v_kernel(
         for m in range(BLOCKS):
             if m + 1 < BLOCKS:
                 finish_dv(m + 1)
-            quantise_dv(m)
-            multiply(m)
+            for cc in range(PASSES):
+                quantise_dv(m, cc)
+                multiply(m, cc)
             store(m)

@@ -23,18 +23,19 @@ HALVES = COLS // N_TILE
 RUN = 4
 
 FLOPS = 2 * ROWS * COLS * COLS
-BYTES = 4 * ROWS * COLS * 2 + 2 * ROWS * COLS * 4 + COLS * COLS * 4 + COLS * 2 + ROWS * 4
+BYTES = 4 * ROWS * COLS * 2 + 3 * ROWS * COLS * 4 + COLS * 2 + ROWS * 4
 
 
 def by_group(matrix):
-    return matrix.rearrange("(c p j) w -> p c j w", c=PASSES, p=P, j=PACK)
+    return matrix.rearrange("(s p j) w -> p s j w", s=PASSES, p=P, j=PACK)
 
 
-def regroup(nc, grouped, rows):
-    nc.scalar.copy(
-        out=grouped.rearrange("p (q i) j -> p q j i", i=RUN),
-        in_=rows.rearrange("p j (q i) -> p q j i", i=RUN),
-    )
+def rows_in_runs(rows):
+    return rows.rearrange("p j (q i) -> p q j i", i=RUN)
+
+
+def grouped_in_runs(grouped):
+    return grouped.rearrange("p (q i) j -> p q j i", i=RUN)
 
 
 def tile_layernormgrucell_pb_v_kernel(
@@ -50,19 +51,19 @@ def tile_layernormgrucell_pb_v_kernel(
         tc.psum_pool(name="spread", bufs=1) as spread,
         tc.psum_pool(name="banks", bufs=6) as banks,
     ):
-        u_sb = resident.tile([P, GROUPS, COLS], F32)
-        xn_sb = resident.tile([P, GROUPS, COLS], F32)
+        u_to_r = resident.tile([P, GROUPS, COLS], F32)
+        xn_to_shift = resident.tile([P, GROUPS, COLS], F32)
         h_sb = resident.tile([P, GROUPS, COLS], BF16)
         c_sb = resident.tile([P, GROUPS, COLS], BF16)
-        g_sb = resident.tile([P, GROUPS, COLS], BF16)
+        grad_sb = resident.tile([P, GROUPS, COLS], BF16)
         x_sb = resident.tile([P, GROUPS, COLS], BF16)
         x_grouped = resident.tile([P, PASSES, COLS, PACK], BF16, align_bytes=64)
         x_codes = resident.tile([P, PASSES, COLS], U32, align_bytes=64)
         x_scales = resident.tile([P, PASSES, COLS], U8, align_bytes=64)
         rstd_sb = resident.tile([P, GROUPS], F32)
-        sum_dn = resident.tile([P, GROUPS], F32)
-        mean_dn = resident.tile([P, GROUPS], F32)
-        mean_dn_xn = resident.tile([P, GROUPS], F32)
+        sum_r = resident.tile([P, GROUPS], F32)
+        mean_r = resident.tile([P, GROUPS], F32)
+        mean_r_xn = resident.tile([P, GROUPS], F32)
         gamma_row = resident.tile([P, COLS], BF16)
         ones = resident.tile([P, P], BF16)
         gamma_sb = resident.tile([P, COLS], BF16)
@@ -70,119 +71,121 @@ def tile_layernormgrucell_pb_v_kernel(
         def load(tile_sb, matrix, g):
             nc.sync.dma_start(out=tile_sb[:, g, :], in_=by_group(matrix)[:, g // PACK, g % PACK, :])
 
-        def load_pair(first):
-            pair = (first, first + 1)
+        def load_pair(pair):
             for g in pair:
                 load(h_sb, h, g)
                 load(c_sb, c, g)
-            for tile_sb, matrix in ((u_sb, u), (g_sb, grad_out), (xn_sb, xn)):
+            for tile_sb, matrix in ((u_to_r, u), (grad_sb, grad_out), (xn_to_shift, xn)):
                 for g in pair:
                     load(tile_sb, matrix, g)
 
-        load_pair(0)
-        load_pair(2)
+        load_pair((0, 1))
+        load_pair((2, 3))
         for g in range(GROUPS):
             load(x_sb, x, g)
-        load_pair(4)
-        load_pair(6)
+        load_pair((4, 5))
+        load_pair((6, 7))
 
         nc.vector.memset(gamma_row[:].bitcast(I32), 0)
         nc.vector.memset(ones[:], 1.0)
         nc.scalar.dma_start(out=gamma_row[0:1, :], in_=ln_gamma[1:2, :])
         nc.scalar.dma_start(
-            out=rstd_sb[:].rearrange("p (c j) -> p c j", j=PACK),
-            in_=rstd.rearrange("(c p j) o -> p c (j o)", c=PASSES, p=P, j=PACK),
+            out=rstd_sb[:].rearrange("p (s j) -> p s j", j=PACK),
+            in_=rstd.rearrange("(s p j) o -> p s (j o)", s=PASSES, p=P, j=PACK),
         )
         gamma_ps = spread.tile([P, COLS], BF16)
         for n in range(HALVES):
-            cols = slice(n * N_TILE, (n + 1) * N_TILE)
-            nc.tensor.matmul(out=gamma_ps[:, cols], lhsT=ones[:], rhs=gamma_row[:, cols], start=True, stop=True)
+            half = slice(n * N_TILE, (n + 1) * N_TILE)
+            nc.tensor.matmul(out=gamma_ps[:, half], lhsT=ones[:], rhs=gamma_row[:, half], start=True, stop=True)
         nc.scalar.copy(out=gamma_sb[:], in_=gamma_ps[:])
 
-        def chain(pair):
+        def r_and_shift(pair):
             diff = {}
             for g in pair:
                 diff[g] = scratch.tile([P, COLS], F32, name="diff")
                 nc.vector.tensor_tensor(out=diff[g][:], in0=h_sb[:, g, :], in1=c_sb[:, g, :], op=ALU.subtract)
             for g in pair:
                 nc.vector.scalar_tensor_tensor(
-                    out=u_sb[:, g, :], in0=u_sb[:, g, :], scalar=1.0, in1=u_sb[:, g, :],
+                    out=u_to_r[:, g, :], in0=u_to_r[:, g, :], scalar=1.0, in1=u_to_r[:, g, :],
                     op0=ALU.subtract, op1=ALU.mult,
                 )
             for g in pair:
-                nc.vector.tensor_tensor(out=u_sb[:, g, :], in0=u_sb[:, g, :], in1=diff[g][:], op=ALU.mult)
+                nc.vector.tensor_tensor(out=u_to_r[:, g, :], in0=u_to_r[:, g, :], in1=diff[g][:], op=ALU.mult)
             for g in pair:
-                nc.vector.tensor_tensor(out=u_sb[:, g, :], in0=u_sb[:, g, :], in1=g_sb[:, g, :], op=ALU.mult)
+                nc.vector.tensor_tensor(out=u_to_r[:, g, :], in0=u_to_r[:, g, :], in1=grad_sb[:, g, :], op=ALU.mult)
             for g in pair:
                 nc.vector.scalar_tensor_tensor(
-                    out=u_sb[:, g, :], in0=u_sb[:, g, :], scalar=rstd_sb[:, g : g + 1], in1=gamma_sb[:],
-                    op0=ALU.mult, op1=ALU.mult, accum_out=sum_dn[:, g : g + 1],
+                    out=u_to_r[:, g, :], in0=u_to_r[:, g, :], scalar=rstd_sb[:, g : g + 1], in1=gamma_sb[:],
+                    op0=ALU.mult, op1=ALU.mult, accum_out=sum_r[:, g : g + 1],
                 )
             for g in pair:
                 nc.vector.scalar_tensor_tensor(
-                    out=diff[g][:], in0=u_sb[:, g, :], scalar=1.0 / COLS, in1=xn_sb[:, g, :],
-                    op0=ALU.mult, op1=ALU.mult, accum_out=mean_dn_xn[:, g : g + 1],
+                    out=diff[g][:], in0=u_to_r[:, g, :], scalar=1.0 / COLS, in1=xn_to_shift[:, g, :],
+                    op0=ALU.mult, op1=ALU.mult, accum_out=mean_r_xn[:, g : g + 1],
                 )
             for g in pair:
-                nc.scalar.mul(out=mean_dn[:, g : g + 1], in_=sum_dn[:, g : g + 1], mul=1.0 / COLS)
+                nc.scalar.mul(out=mean_r[:, g : g + 1], in_=sum_r[:, g : g + 1], mul=1.0 / COLS)
             for g in pair:
                 nc.scalar.activation(
-                    out=xn_sb[:, g, :], in_=xn_sb[:, g, :], func=ACT.Identity,
-                    scale=mean_dn_xn[:, g : g + 1], bias=mean_dn[:, g : g + 1],
+                    out=xn_to_shift[:, g, :], in_=xn_to_shift[:, g, :], func=ACT.Identity,
+                    scale=mean_r_xn[:, g : g + 1], bias=mean_r[:, g : g + 1],
                 )
 
-        chain((0, 1))
-        for cc in range(PASSES):
+        r_and_shift((0, 1))
+        for s in range(PASSES):
             for n in range(HALVES):
-                cols = slice(n * N_TILE, (n + 1) * N_TILE)
-                regroup(nc, x_grouped[:, cc, cols, :], x_sb[:, cc * PACK : (cc + 1) * PACK, cols])
-        chain((2, 3))
-        chain((4, 5))
-        chain((6, 7))
-        for cc in range(PASSES):
+                half = slice(n * N_TILE, (n + 1) * N_TILE)
+                nc.scalar.copy(
+                    out=grouped_in_runs(x_grouped[:, s, half, :]),
+                    in_=rows_in_runs(x_sb[:, s * PACK : (s + 1) * PACK, half]),
+                )
+        r_and_shift((2, 3))
+        r_and_shift((4, 5))
+        r_and_shift((6, 7))
+        for s in range(PASSES):
             nc.vector.quantize_mx(
-                out=x_codes[:, cc, :].bitcast(E4M3_X4),
-                scales=x_scales[:, cc, :],
-                in_=x_grouped[:, cc, :, :].rearrange("p w j -> p (w j)"),
+                out=x_codes[:, s, :].bitcast(E4M3_X4),
+                scales=x_scales[:, s, :],
+                in_=x_grouped[:, s, :, :].rearrange("p w j -> p (w j)"),
             )
 
         dv_grouped, dv_codes, dv_scales, acc = {}, {}, {}, {}
 
         def finish_dv(m):
-            cols = slice(m * M_TILE, (m + 1) * M_TILE)
+            dv_cols = slice(m * M_TILE, (m + 1) * M_TILE)
             dv_grouped[m] = block.tile([P, PASSES, M_TILE, PACK], BF16, name="dv_grouped", align_bytes=64)
-            for cc in range(PASSES):
-                groups = slice(cc * PACK, (cc + 1) * PACK)
+            for s in range(PASSES):
+                groups = slice(s * PACK, (s + 1) * PACK)
                 nc.vector.tensor_tensor(
-                    out=dv_grouped[m][:, cc, :, :].rearrange("p (q i) j -> p q j i", i=RUN),
-                    in0=u_sb[:, groups, cols].rearrange("p j (q i) -> p q j i", i=RUN),
-                    in1=xn_sb[:, groups, cols].rearrange("p j (q i) -> p q j i", i=RUN),
+                    out=grouped_in_runs(dv_grouped[m][:, s, :, :]),
+                    in0=rows_in_runs(u_to_r[:, groups, dv_cols]),
+                    in1=rows_in_runs(xn_to_shift[:, groups, dv_cols]),
                     op=ALU.subtract,
                 )
 
-        def quantise_dv(m, cc):
-            if cc == 0:
+        def quantise_dv(m, s):
+            if s == 0:
                 dv_codes[m] = block.tile([P, PASSES, M_TILE], U32, name="dv_codes", align_bytes=64)
                 dv_scales[m] = block.tile([P, PASSES, M_TILE], U8, name="dv_scales", align_bytes=64)
             nc.vector.quantize_mx(
-                out=dv_codes[m][:, cc, :].bitcast(E5M2_X4),
-                scales=dv_scales[m][:, cc, :],
-                in_=dv_grouped[m][:, cc, :, :].rearrange("p w j -> p (w j)"),
+                out=dv_codes[m][:, s, :].bitcast(E5M2_X4),
+                scales=dv_scales[m][:, s, :],
+                in_=dv_grouped[m][:, s, :, :].rearrange("p w j -> p (w j)"),
             )
 
-        def multiply(m, cc):
+        def multiply(m, s):
             for n in range(HALVES):
-                cols = slice(n * N_TILE, (n + 1) * N_TILE)
-                if cc == 0:
+                half = slice(n * N_TILE, (n + 1) * N_TILE)
+                if s == 0:
                     acc[m, n] = banks.tile([P, N_TILE], F32, name="acc")
                 nc.tensor.matmul_mx(
                     out=acc[m, n][:],
-                    lhsT=dv_codes[m][:, cc, :].bitcast(E5M2_X4),
-                    lhsT_scale=dv_scales[m][:, cc, :],
-                    rhs=x_codes[:, cc, cols].bitcast(E4M3_X4),
-                    rhs_scale=x_scales[:, cc, cols],
-                    start=(cc == 0),
-                    stop=(cc == PASSES - 1),
+                    lhsT=dv_codes[m][:, s, :].bitcast(E5M2_X4),
+                    lhsT_scale=dv_scales[m][:, s, :],
+                    rhs=x_codes[:, s, half].bitcast(E4M3_X4),
+                    rhs_scale=x_scales[:, s, half],
+                    start=(s == 0),
+                    stop=(s == PASSES - 1),
                 )
 
         def store(m):
@@ -197,7 +200,7 @@ def tile_layernormgrucell_pb_v_kernel(
         for m in range(BLOCKS):
             if m + 1 < BLOCKS:
                 finish_dv(m + 1)
-            for cc in range(PASSES):
-                quantise_dv(m, cc)
-                multiply(m, cc)
+            for s in range(PASSES):
+                quantise_dv(m, s)
+                multiply(m, s)
             store(m)

@@ -75,7 +75,8 @@ def tile_layernormgrucell_pb_v_kernel(
             for g in pair:
                 load(h_sb, h, g)
                 load(c_sb, c, g)
-            for tile_sb, matrix in ((u_to_r, u), (grad_sb, grad_out), (xn_to_shift, xn)):
+                load(u_to_r, u, g)
+            for tile_sb, matrix in ((grad_sb, grad_out), (xn_to_shift, xn)):
                 for g in pair:
                     load(tile_sb, matrix, g)
 
@@ -99,18 +100,20 @@ def tile_layernormgrucell_pb_v_kernel(
             nc.tensor.matmul(out=gamma_ps[:, half], lhsT=ones[:], rhs=gamma_row[:, half], start=True, stop=True)
         nc.scalar.copy(out=gamma_sb[:], in_=gamma_ps[:])
 
-        def r_and_shift(pair):
+        def square(pair):
+            for g in pair:
+                nc.scalar.activation(out=u_to_r[:, g, :], in_=u_to_r[:, g, :], func=ACT.Square, bias=-0.5, scale=1.0)
+
+        def make_r(pair):
             diff = {}
             for g in pair:
                 diff[g] = scratch.tile([P, COLS], F32, name="diff")
                 nc.vector.tensor_tensor(out=diff[g][:], in0=h_sb[:, g, :], in1=c_sb[:, g, :], op=ALU.subtract)
             for g in pair:
                 nc.vector.scalar_tensor_tensor(
-                    out=u_to_r[:, g, :], in0=u_to_r[:, g, :], scalar=1.0, in1=u_to_r[:, g, :],
+                    out=u_to_r[:, g, :], in0=u_to_r[:, g, :], scalar=0.25, in1=diff[g][:],
                     op0=ALU.subtract, op1=ALU.mult,
                 )
-            for g in pair:
-                nc.vector.tensor_tensor(out=u_to_r[:, g, :], in0=u_to_r[:, g, :], in1=diff[g][:], op=ALU.mult)
             for g in pair:
                 nc.vector.tensor_tensor(out=u_to_r[:, g, :], in0=u_to_r[:, g, :], in1=grad_sb[:, g, :], op=ALU.mult)
             for g in pair:
@@ -123,6 +126,8 @@ def tile_layernormgrucell_pb_v_kernel(
                     out=diff[g][:], in0=u_to_r[:, g, :], scalar=1.0 / COLS, in1=xn_to_shift[:, g, :],
                     op0=ALU.mult, op1=ALU.mult, accum_out=mean_r_xn[:, g : g + 1],
                 )
+
+        def make_shift(pair):
             for g in pair:
                 nc.scalar.mul(out=mean_r[:, g : g + 1], in_=sum_r[:, g : g + 1], mul=1.0 / COLS)
             for g in pair:
@@ -131,17 +136,28 @@ def tile_layernormgrucell_pb_v_kernel(
                     scale=mean_r_xn[:, g : g + 1], bias=mean_r[:, g : g + 1],
                 )
 
-        r_and_shift((0, 1))
-        for s in range(PASSES):
+        def regroup_x(s):
             for n in range(HALVES):
                 half = slice(n * N_TILE, (n + 1) * N_TILE)
                 nc.scalar.copy(
                     out=grouped_in_runs(x_grouped[:, s, half, :]),
                     in_=rows_in_runs(x_sb[:, s * PACK : (s + 1) * PACK, half]),
                 )
-        r_and_shift((2, 3))
-        r_and_shift((4, 5))
-        r_and_shift((6, 7))
+
+        square((0, 1))
+        make_r((0, 1))
+        square((2, 3))
+        make_shift((0, 1))
+        make_r((2, 3))
+        regroup_x(0)
+        square((4, 5))
+        make_shift((2, 3))
+        make_r((4, 5))
+        regroup_x(1)
+        square((6, 7))
+        make_shift((4, 5))
+        make_r((6, 7))
+        make_shift((6, 7))
         for s in range(PASSES):
             nc.vector.quantize_mx(
                 out=x_codes[:, s, :].bitcast(E4M3_X4),

@@ -75,8 +75,7 @@ def tile_layernormgrucell_pb_v_kernel(
             for g in pair:
                 load(h_sb, h, g)
                 load(c_sb, c, g)
-                load(u_to_r, u, g)
-            for tile_sb, matrix in ((grad_sb, grad_out), (xn_to_shift, xn)):
+            for tile_sb, matrix in ((u_to_r, u), (grad_sb, grad_out), (xn_to_shift, xn)):
                 for g in pair:
                     load(tile_sb, matrix, g)
 
@@ -98,7 +97,6 @@ def tile_layernormgrucell_pb_v_kernel(
         for n in range(HALVES):
             half = slice(n * N_TILE, (n + 1) * N_TILE)
             nc.tensor.matmul(out=gamma_ps[:, half], lhsT=ones[:], rhs=gamma_row[:, half], start=True, stop=True)
-        nc.scalar.copy(out=gamma_sb[:], in_=gamma_ps[:])
 
         def square(pair):
             for g in pair:
@@ -145,6 +143,7 @@ def tile_layernormgrucell_pb_v_kernel(
                 )
 
         square((0, 1))
+        nc.scalar.copy(out=gamma_sb[:], in_=gamma_ps[:])
         make_r((0, 1))
         square((2, 3))
         make_shift((0, 1))

@@ -1,4 +1,5 @@
 import concourse.mybir as mybir
+from concourse.masks import make_identity
 
 F32 = mybir.dt.float32
 BF16 = mybir.dt.bfloat16
@@ -46,10 +47,10 @@ def tile_layernormgrucell_pb_v_kernel(
         tc.manual_schedule(),
         tc.tile_pool(name="resident", bufs=1) as resident,
         tc.tile_pool(name="scratch", bufs=4) as scratch,
-        tc.tile_pool(name="block", bufs=3) as block,
+        tc.tile_pool(name="turned", bufs=3) as turned,
+        tc.tile_pool(name="block", bufs=4) as block,
         tc.tile_pool(name="result", bufs=6) as result,
-        tc.psum_pool(name="spread", bufs=1) as spread,
-        tc.psum_pool(name="banks", bufs=6) as banks,
+        tc.psum_pool(name="banks", bufs=8) as banks,
     ):
         u_to_r = resident.tile([P, GROUPS, COLS], F32)
         xn_to_shift = resident.tile([P, GROUPS, COLS], F32)
@@ -60,143 +61,204 @@ def tile_layernormgrucell_pb_v_kernel(
         x_grouped = resident.tile([P, PASSES, COLS, PACK], BF16, align_bytes=64)
         x_codes = resident.tile([P, PASSES, COLS], U32, align_bytes=64)
         x_scales = resident.tile([P, PASSES, COLS], U8, align_bytes=64)
+        dv_codes = resident.tile([P, PASSES, COLS], U32, align_bytes=64)
+        dv_scales = resident.tile([P, PASSES, COLS], U8, align_bytes=64)
         rstd_sb = resident.tile([P, GROUPS], F32)
+        sum_r_half = resident.tile([P, GROUPS, HALVES], F32)
         sum_r = resident.tile([P, GROUPS], F32)
         mean_r = resident.tile([P, GROUPS], F32)
         mean_r_xn = resident.tile([P, GROUPS], F32)
-        gamma_row = resident.tile([P, COLS], BF16)
-        ones = resident.tile([P, P], BF16)
-        gamma_sb = resident.tile([P, COLS], BF16)
+        gamma_rows = resident.tile([P, P], BF16)
+        gamma_col = resident.tile([P, BLOCKS], F32)
+        ident_bf = resident.tile([P, P], BF16)
+        ident_f32 = resident.tile([P, P], F32)
+        warm = resident.tile([P, 2], F32)
+        ident_neg = resident.tile([P, P], BF16)
 
-        def load(tile_sb, matrix, g):
-            nc.sync.dma_start(out=tile_sb[:, g, :], in_=by_group(matrix)[:, g // PACK, g % PACK, :])
-
-        def load_pair(pair):
-            for g in pair:
-                load(h_sb, h, g)
-                load(c_sb, c, g)
-            for tile_sb, matrix in ((u_to_r, u), (grad_sb, grad_out), (xn_to_shift, xn)):
-                for g in pair:
-                    load(tile_sb, matrix, g)
-
-        load_pair((0, 1))
-        load_pair((2, 3))
-        for g in range(GROUPS):
-            load(x_sb, x, g)
-        load_pair((4, 5))
-        load_pair((6, 7))
-
-        nc.vector.memset(gamma_row[:].bitcast(I32), 0)
-        nc.vector.memset(ones[:], 1.0)
-        nc.scalar.dma_start(out=gamma_row[0:1, :], in_=ln_gamma[1:2, :])
+        nc.vector.memset(gamma_rows[:].bitcast(I32), 0)
+        nc.scalar.dma_start(out=gamma_rows[0:BLOCKS, :], in_=ln_gamma[1:2, :].rearrange("o (b p) -> (o b) p", p=P))
         nc.scalar.dma_start(
             out=rstd_sb[:].rearrange("p (s j) -> p s j", j=PACK),
             in_=rstd.rearrange("(s p j) o -> p s (j o)", s=PASSES, p=P, j=PACK),
         )
-        gamma_ps = spread.tile([P, COLS], BF16)
-        for n in range(HALVES):
-            half = slice(n * N_TILE, (n + 1) * N_TILE)
-            nc.tensor.matmul(out=gamma_ps[:, half], lhsT=ones[:], rhs=gamma_row[:, half], start=True, stop=True)
+        nc.vector.memset(warm[:], 0.0)
+        nc.scalar.activation(out=warm[:, 1:2], in_=warm[:, 0:1], func=ACT.Square)
+        make_identity(nc, ident_bf[:])
+        make_identity(nc, ident_f32[:])
+        nc.scalar.mul(out=ident_neg[:], in_=ident_bf[:], mul=-1.0)
 
-        def square(pair):
-            for g in pair:
+        def load(tile_sb, matrix, g):
+            nc.sync.dma_start(out=tile_sb[:, g, :], in_=by_group(matrix)[:, g // PACK, g % PACK, :])
+
+        def load_h_c(k):
+            for g in (2 * k, 2 * k + 1):
+                load(h_sb, h, g)
+                load(c_sb, c, g)
+
+        def load_both(tile_sb, matrix, k):
+            for g in (2 * k, 2 * k + 1):
+                load(tile_sb, matrix, g)
+
+        def load_x(s):
+            for g in range(s * PACK, (s + 1) * PACK):
+                load(x_sb, x, g)
+
+        load_h_c(0)
+        load_both(u_to_r, u, 0)
+        load_both(grad_sb, grad_out, 0)
+        for k in range(1, 4):
+            if k == 2:
+                load_x(0)
+            load_h_c(k)
+            load_both(xn_to_shift, xn, k - 1)
+            load_both(u_to_r, u, k)
+            if k == 3:
+                load_x(1)
+            load_both(grad_sb, grad_out, k)
+        load_both(xn_to_shift, xn, 3)
+
+        gamma_ps = banks.tile([P, P], BF16, name="bank")
+        nc.tensor.transpose(out=gamma_ps[:], in_=gamma_rows[:], identity=ident_bf[:])
+
+        grad_t, grad_gamma_t, grad_gamma = {}, {}, {}
+
+        def square(k):
+            for g in (2 * k, 2 * k + 1):
                 nc.scalar.activation(out=u_to_r[:, g, :], in_=u_to_r[:, g, :], func=ACT.Square, bias=-0.5, scale=1.0)
 
-        def make_r(pair):
-            diff = {}
-            for g in pair:
-                diff[g] = scratch.tile([P, COLS], F32, name="diff")
-                nc.vector.tensor_tensor(out=diff[g][:], in0=h_sb[:, g, :], in1=c_sb[:, g, :], op=ALU.subtract)
-            for g in pair:
+        def turn(k, n):
+            grad_t[k, n] = banks.tile([P, 4, 2, P], BF16, name="bank")
+            for b in range(4):
+                for i in range(2):
+                    first = (4 * n + b) * P
+                    nc.tensor.transpose(
+                        out=grad_t[k, n][:, b, i, :], in_=grad_sb[:, 2 * k + i, first : first + P], identity=ident_bf[:]
+                    )
+
+        def times_gamma(k, n):
+            grad_gamma_t[k, n] = turned.tile([P, 4, 2, P], F32, name="grad_gamma_t")
+            for b in range(4):
+                nc.scalar.activation(
+                    out=grad_gamma_t[k, n][:, b, :, :], in_=grad_t[k, n][:, b, :, :], func=ACT.Copy,
+                    scale=gamma_col[:, 4 * n + b : 4 * n + b + 1],
+                )
+
+        def turn_back(k, n):
+            for i in range(2):
+                grad_gamma[2 * k + i, n] = banks.tile([P, N_TILE], F32, name="bank")
+                for b in range(4):
+                    nc.tensor.transpose(
+                        out=grad_gamma[2 * k + i, n][:, b * P : (b + 1) * P], in_=grad_gamma_t[k, n][:, b, i, :],
+                        identity=ident_f32[:],
+                    )
+
+        diff, diff_ps = {}, {}
+
+        def subtract(g):
+            diff[g] = scratch.tile([P, COLS], F32, name="diff")
+            nc.vector.tensor_tensor(out=diff[g][:], in0=h_sb[:, g, :], in1=c_sb[:, g, :], op=ALU.subtract)
+
+        def subtract_on_tensor(g):
+            for n in range(HALVES):
+                half = slice(n * N_TILE, (n + 1) * N_TILE)
+                diff_ps[g, n] = banks.tile([P, N_TILE], F32, name="bank")
+                nc.tensor.matmul(out=diff_ps[g, n][:], lhsT=ident_bf[:], rhs=h_sb[:, g, half], start=True, stop=False)
+                nc.tensor.matmul(out=diff_ps[g, n][:], lhsT=ident_neg[:], rhs=c_sb[:, g, half], start=False, stop=True)
+
+        def times_gate(g):
+            if g in diff:
                 nc.vector.scalar_tensor_tensor(
                     out=u_to_r[:, g, :], in0=u_to_r[:, g, :], scalar=0.25, in1=diff[g][:],
                     op0=ALU.subtract, op1=ALU.mult,
                 )
-            for g in pair:
-                nc.vector.tensor_tensor(out=u_to_r[:, g, :], in0=u_to_r[:, g, :], in1=grad_sb[:, g, :], op=ALU.mult)
-            for g in pair:
+            else:
+                for n in range(HALVES):
+                    half = slice(n * N_TILE, (n + 1) * N_TILE)
+                    nc.vector.scalar_tensor_tensor(
+                        out=u_to_r[:, g, half], in0=u_to_r[:, g, half], scalar=0.25, in1=diff_ps[g, n][:],
+                        op0=ALU.subtract, op1=ALU.mult,
+                    )
+
+        def times_grad(k):
+            for n in range(HALVES):
+                half = slice(n * N_TILE, (n + 1) * N_TILE)
+                for g in (2 * k, 2 * k + 1):
+                    nc.vector.scalar_tensor_tensor(
+                        out=u_to_r[:, g, half], in0=u_to_r[:, g, half], scalar=rstd_sb[:, g : g + 1],
+                        in1=grad_gamma[g, n][:], op0=ALU.mult, op1=ALU.mult, accum_out=sum_r_half[:, g, n : n + 1],
+                    )
+
+        def means(k):
+            for g in (2 * k, 2 * k + 1):
+                junk = scratch.tile([P, COLS], F32, name="diff")
                 nc.vector.scalar_tensor_tensor(
-                    out=u_to_r[:, g, :], in0=u_to_r[:, g, :], scalar=rstd_sb[:, g : g + 1], in1=gamma_sb[:],
-                    op0=ALU.mult, op1=ALU.mult, accum_out=sum_r[:, g : g + 1],
-                )
-            for g in pair:
-                nc.vector.scalar_tensor_tensor(
-                    out=diff[g][:], in0=u_to_r[:, g, :], scalar=1.0 / COLS, in1=xn_to_shift[:, g, :],
+                    out=junk[:], in0=u_to_r[:, g, :], scalar=1.0 / COLS, in1=xn_to_shift[:, g, :],
                     op0=ALU.mult, op1=ALU.mult, accum_out=mean_r_xn[:, g : g + 1],
                 )
+            both = slice(2 * k, 2 * k + 2)
+            nc.vector.tensor_reduce(out=sum_r[:, both], in_=sum_r_half[:, both, :], axis=mybir.AxisListType.X, op=ALU.add)
+            nc.vector.tensor_scalar(out=mean_r[:, both], in0=sum_r[:, both], scalar1=1.0 / COLS, scalar2=None, op0=ALU.mult)
 
-        def make_shift(pair):
-            for g in pair:
-                nc.scalar.mul(out=mean_r[:, g : g + 1], in_=sum_r[:, g : g + 1], mul=1.0 / COLS)
-            for g in pair:
+        def make_shift(k):
+            for g in (2 * k, 2 * k + 1):
                 nc.scalar.activation(
                     out=xn_to_shift[:, g, :], in_=xn_to_shift[:, g, :], func=ACT.Identity,
                     scale=mean_r_xn[:, g : g + 1], bias=mean_r[:, g : g + 1],
                 )
 
-        def regroup_x(s):
-            for n in range(HALVES):
-                half = slice(n * N_TILE, (n + 1) * N_TILE)
-                nc.scalar.copy(
-                    out=grouped_in_runs(x_grouped[:, s, half, :]),
-                    in_=rows_in_runs(x_sb[:, s * PACK : (s + 1) * PACK, half]),
-                )
+        def regroup_x(s, n):
+            half = slice(n * N_TILE, (n + 1) * N_TILE)
+            nc.scalar.copy(
+                out=grouped_in_runs(x_grouped[:, s, half, :]),
+                in_=rows_in_runs(x_sb[:, s * PACK : (s + 1) * PACK, half]),
+            )
 
-        square((0, 1))
-        nc.scalar.copy(out=gamma_sb[:], in_=gamma_ps[:])
-        make_r((0, 1))
-        square((2, 3))
-        make_shift((0, 1))
-        make_r((2, 3))
-        regroup_x(0)
-        square((4, 5))
-        make_shift((2, 3))
-        make_r((4, 5))
-        regroup_x(1)
-        square((6, 7))
-        make_shift((4, 5))
-        make_r((6, 7))
-        make_shift((6, 7))
-        for s in range(PASSES):
+        def quantise_x(s):
             nc.vector.quantize_mx(
                 out=x_codes[:, s, :].bitcast(E4M3_X4),
                 scales=x_scales[:, s, :],
                 in_=x_grouped[:, s, :, :].rearrange("p w j -> p (w j)"),
             )
 
-        dv_grouped, dv_codes, dv_scales, acc = {}, {}, {}, {}
+        dv_grouped, acc = {}, {}
 
-        def finish_dv(m):
+        def late_shift(m):
             dv_cols = slice(m * M_TILE, (m + 1) * M_TILE)
-            dv_grouped[m] = block.tile([P, PASSES, M_TILE, PACK], BF16, name="dv_grouped", align_bytes=64)
-            for s in range(PASSES):
-                groups = slice(s * PACK, (s + 1) * PACK)
-                nc.vector.tensor_tensor(
-                    out=grouped_in_runs(dv_grouped[m][:, s, :, :]),
-                    in0=rows_in_runs(u_to_r[:, groups, dv_cols]),
-                    in1=rows_in_runs(xn_to_shift[:, groups, dv_cols]),
-                    op=ALU.subtract,
+            for g in range(PACK, GROUPS):
+                nc.vector.tensor_scalar(
+                    out=xn_to_shift[:, g, dv_cols], in0=xn_to_shift[:, g, dv_cols],
+                    scalar1=mean_r_xn[:, g : g + 1], scalar2=mean_r[:, g : g + 1], op0=ALU.mult, op1=ALU.add,
                 )
 
+        def finish_dv(m, s):
+            dv_cols = slice(m * M_TILE, (m + 1) * M_TILE)
+            groups = slice(s * PACK, (s + 1) * PACK)
+            dv_grouped[m, s] = block.tile([P, M_TILE, PACK], BF16, name="dv_grouped", align_bytes=64)
+            nc.vector.tensor_tensor(
+                out=grouped_in_runs(dv_grouped[m, s][:]),
+                in0=rows_in_runs(u_to_r[:, groups, dv_cols]),
+                in1=rows_in_runs(xn_to_shift[:, groups, dv_cols]),
+                op=ALU.subtract,
+            )
+
         def quantise_dv(m, s):
-            if s == 0:
-                dv_codes[m] = block.tile([P, PASSES, M_TILE], U32, name="dv_codes", align_bytes=64)
-                dv_scales[m] = block.tile([P, PASSES, M_TILE], U8, name="dv_scales", align_bytes=64)
+            dv_cols = slice(m * M_TILE, (m + 1) * M_TILE)
             nc.vector.quantize_mx(
-                out=dv_codes[m][:, s, :].bitcast(E5M2_X4),
-                scales=dv_scales[m][:, s, :],
-                in_=dv_grouped[m][:, s, :, :].rearrange("p w j -> p (w j)"),
+                out=dv_codes[:, s, dv_cols].bitcast(E5M2_X4),
+                scales=dv_scales[:, s, dv_cols],
+                in_=dv_grouped[m, s][:].rearrange("p w j -> p (w j)"),
             )
 
         def multiply(m, s):
+            dv_cols = slice(m * M_TILE, (m + 1) * M_TILE)
             for n in range(HALVES):
                 half = slice(n * N_TILE, (n + 1) * N_TILE)
                 if s == 0:
-                    acc[m, n] = banks.tile([P, N_TILE], F32, name="acc")
+                    acc[m, n] = banks.tile([P, N_TILE], F32, name="bank")
                 nc.tensor.matmul_mx(
                     out=acc[m, n][:],
-                    lhsT=dv_codes[m][:, s, :].bitcast(E5M2_X4),
-                    lhsT_scale=dv_scales[m][:, s, :],
+                    lhsT=dv_codes[:, s, dv_cols].bitcast(E5M2_X4),
+                    lhsT_scale=dv_scales[:, s, dv_cols],
                     rhs=x_codes[:, s, half].bitcast(E4M3_X4),
                     rhs_scale=x_scales[:, s, half],
                     start=(s == 0),
@@ -211,11 +273,71 @@ def tile_layernormgrucell_pb_v_kernel(
                     out=out[m * M_TILE : (m + 1) * M_TILE, n * N_TILE : (n + 1) * N_TILE], in_=out_sb[:]
                 )
 
-        finish_dv(0)
+        ON_TENSOR = (4, 5, 6)
+
+        def start_pair(k):
+            for g in (2 * k, 2 * k + 1):
+                if g in ON_TENSOR:
+                    subtract_on_tensor(g)
+                else:
+                    subtract(g)
+
+        def gates(k):
+            for g in (2 * k, 2 * k + 1):
+                times_gate(g)
+
+        def early_dv(blocks):
+            finish_dv(blocks[0], 0)
+            for i, m in enumerate(blocks):
+                if i + 1 < len(blocks):
+                    finish_dv(blocks[i + 1], 0)
+                quantise_dv(m, 0)
+
+        square(0)
+        nc.scalar.copy(out=gamma_col[:], in_=gamma_ps[:, 0:BLOCKS])
+        start_pair(0)
+        turn(0, 0)
+        turn(0, 1)
+        gates(0)
+        for k in range(4):
+            for n in range(HALVES):
+                times_gamma(k, n)
+                turn_back(k, n)
+            if k == 1:
+                make_shift(0)
+                regroup_x(0, 0)
+            if k == 2:
+                regroup_x(0, 1)
+                make_shift(1)
+            if k == 3:
+                regroup_x(1, 0)
+                regroup_x(1, 1)
+            if k + 1 < 4:
+                start_pair(k + 1)
+                square(k + 1)
+                turn(k + 1, 0)
+                turn(k + 1, 1)
+            times_grad(k)
+            means(k)
+            if k == 2:
+                quantise_x(0)
+                early_dv((0, 1, 2, 3))
+            if k + 1 < 4:
+                gates(k + 1)
+        for m in range(4):
+            multiply(m, 0)
+        quantise_x(1)
+        late_shift(0)
+        late_shift(1)
+        finish_dv(0, 1)
         for m in range(BLOCKS):
+            if m + 2 < BLOCKS:
+                late_shift(m + 2)
             if m + 1 < BLOCKS:
-                finish_dv(m + 1)
-            for s in range(PASSES):
-                quantise_dv(m, s)
-                multiply(m, s)
+                finish_dv(m + 1, 1)
+            quantise_dv(m, 1)
+            multiply(m, 1)
+            if 1 <= m and m + 3 < BLOCKS:
+                early_dv((m + 3,))
+                multiply(m + 3, 0)
             store(m)

@@ -87,21 +87,19 @@ def tile_layernormgrucell_pb_v_kernel(
         make_identity(nc, ident_f32[:])
         nc.scalar.mul(out=ident_neg[:], in_=ident_bf[:], mul=-1.0)
 
-        def load(tile_sb, matrix, g):
-            nc.sync.dma_start(out=tile_sb[:, g, :], in_=by_group(matrix)[:, g // PACK, g % PACK, :])
+        def load(tile_sb, matrix, first, count):
+            s, j = first // PACK, first % PACK
+            nc.sync.dma_start(out=tile_sb[:, first : first + count, :], in_=by_group(matrix)[:, s, j : j + count, :])
 
         def load_h_c(k):
-            for g in (2 * k, 2 * k + 1):
-                load(h_sb, h, g)
-                load(c_sb, c, g)
+            load(h_sb, h, 2 * k, 2)
+            load(c_sb, c, 2 * k, 2)
 
         def load_both(tile_sb, matrix, k):
-            for g in (2 * k, 2 * k + 1):
-                load(tile_sb, matrix, g)
+            load(tile_sb, matrix, 2 * k, 2)
 
         def load_x(s):
-            for g in range(s * PACK, (s + 1) * PACK):
-                load(x_sb, x, g)
+            load(x_sb, x, s * PACK, PACK)
 
         load_h_c(0)
         load_both(u_to_r, u, 0)

@@ -101,17 +101,15 @@ def tile_layernormgrucell_pb_v_kernel(
         def load_x(s):
             load(x_sb, x, s * PACK, PACK)
 
+        load_x(0)
+        load_x(1)
         load_h_c(0)
         load_both(u_to_r, u, 0)
         load_both(grad_sb, grad_out, 0)
         for k in range(1, 4):
-            if k == 2:
-                load_x(0)
             load_h_c(k)
             load_both(xn_to_shift, xn, k - 1)
             load_both(u_to_r, u, k)
-            if k == 3:
-                load_x(1)
             load_both(grad_sb, grad_out, k)
         load_both(xn_to_shift, xn, 3)
 
@@ -204,9 +202,10 @@ def tile_layernormgrucell_pb_v_kernel(
                     scale=mean_r_xn[:, g : g + 1], bias=mean_r[:, g : g + 1],
                 )
 
-        def regroup_x(s, n):
+        def regroup_x(s, n, on_scalar):
             half = slice(n * N_TILE, (n + 1) * N_TILE)
-            nc.scalar.copy(
+            copy = nc.scalar.copy if on_scalar else nc.vector.tensor_copy
+            copy(
                 out=grouped_in_runs(x_grouped[:, s, half, :]),
                 in_=rows_in_runs(x_sb[:, s * PACK : (s + 1) * PACK, half]),
             )
@@ -222,7 +221,7 @@ def tile_layernormgrucell_pb_v_kernel(
 
         def late_shift(m):
             dv_cols = slice(m * M_TILE, (m + 1) * M_TILE)
-            for g in range(PACK, GROUPS):
+            for g in (6, 7):
                 nc.vector.tensor_scalar(
                     out=xn_to_shift[:, g, dv_cols], in0=xn_to_shift[:, g, dv_cols],
                     scalar1=mean_r_xn[:, g : g + 1], scalar2=mean_r[:, g : g + 1], op0=ALU.mult, op1=ALU.add,
@@ -291,6 +290,12 @@ def tile_layernormgrucell_pb_v_kernel(
                     finish_dv(blocks[i + 1], 0)
                 quantise_dv(m, 0)
 
+        regroup_x(0, 0, False)
+        regroup_x(0, 1, False)
+        regroup_x(1, 0, True)
+        regroup_x(1, 1, False)
+        quantise_x(0)
+        quantise_x(1)
         square(0)
         nc.scalar.copy(out=gamma_col[:], in_=gamma_ps[:, 0:BLOCKS])
         start_pair(0)
@@ -301,15 +306,8 @@ def tile_layernormgrucell_pb_v_kernel(
             for n in range(HALVES):
                 times_gamma(k, n)
                 turn_back(k, n)
-            if k == 1:
-                make_shift(0)
-                regroup_x(0, 0)
-            if k == 2:
-                regroup_x(0, 1)
-                make_shift(1)
-            if k == 3:
-                regroup_x(1, 0)
-                regroup_x(1, 1)
+            if k >= 1:
+                make_shift(k - 1)
             if k + 1 < 4:
                 start_pair(k + 1)
                 square(k + 1)
@@ -318,13 +316,11 @@ def tile_layernormgrucell_pb_v_kernel(
             times_grad(k)
             means(k)
             if k == 2:
-                quantise_x(0)
                 early_dv((0, 1, 2, 3))
             if k + 1 < 4:
                 gates(k + 1)
         for m in range(4):
             multiply(m, 0)
-        quantise_x(1)
         late_shift(0)
         late_shift(1)
         finish_dv(0, 1)

@@ -321,17 +321,16 @@ def tile_layernormgrucell_pb_v_kernel(
                 gates(k + 1)
         for m in range(4):
             multiply(m, 0)
+        units = [(m, 1) for m in range(4)] + [(m, s) for m in range(4, BLOCKS) for s in range(PASSES)]
         late_shift(0)
         late_shift(1)
         finish_dv(0, 1)
-        for m in range(BLOCKS):
-            if m + 2 < BLOCKS:
+        for i, (m, s) in enumerate(units):
+            if s == 1 and m + 2 < BLOCKS:
                 late_shift(m + 2)
-            if m + 1 < BLOCKS:
-                finish_dv(m + 1, 1)
-            quantise_dv(m, 1)
-            multiply(m, 1)
-            if 1 <= m and m + 3 < BLOCKS:
-                early_dv((m + 3,))
-                multiply(m + 3, 0)
-            store(m)
+            if i + 1 < len(units):
+                finish_dv(units[i + 1][0], units[i + 1][1])
+            quantise_dv(m, s)
+            multiply(m, s)
+            if s == 1:
+                store(m)

@@ -22,6 +22,10 @@ N_TILE = 512
 BLOCKS = COLS // M_TILE
 HALVES = COLS // N_TILE
 RUN = 4
+EARLY_2 = 0
+EARLY_3 = 0
+SHIFT_G = True
+FILL = 2
 
 FLOPS = 2 * ROWS * COLS * COLS
 BYTES = 4 * ROWS * COLS * 2 + 3 * ROWS * COLS * 4 + COLS * 2 + ROWS * 4
@@ -47,7 +51,7 @@ def tile_layernormgrucell_pb_v_kernel(
         tc.manual_schedule(),
         tc.tile_pool(name="resident", bufs=1) as resident,
         tc.tile_pool(name="scratch", bufs=4) as scratch,
-        tc.tile_pool(name="turned", bufs=3) as turned,
+        tc.tile_pool(name="turned", bufs=5) as turned,
         tc.tile_pool(name="block", bufs=4) as block,
         tc.tile_pool(name="result", bufs=6) as result,
         tc.psum_pool(name="banks", bufs=8) as banks,
@@ -70,6 +74,7 @@ def tile_layernormgrucell_pb_v_kernel(
         mean_r_xn = resident.tile([P, GROUPS], F32)
         gamma_rows = resident.tile([P, P], BF16)
         gamma_col = resident.tile([P, BLOCKS], F32)
+        gamma_neg = resident.tile([P, BLOCKS], F32)
         ident_bf = resident.tile([P, P], BF16)
         ident_f32 = resident.tile([P, P], F32)
         warm = resident.tile([P, 2], F32)
@@ -82,6 +87,7 @@ def tile_layernormgrucell_pb_v_kernel(
             in_=rstd.rearrange("(s p j) o -> p s (j o)", s=PASSES, p=P, j=PACK),
         )
         nc.vector.memset(warm[:], 0.0)
+        nc.vector.memset(sum_r_half[:], 0.0)
         nc.scalar.activation(out=warm[:, 1:2], in_=warm[:, 0:1], func=ACT.Square)
         make_identity(nc, ident_bf[:])
         make_identity(nc, ident_f32[:])
@@ -116,50 +122,65 @@ def tile_layernormgrucell_pb_v_kernel(
         gamma_ps = banks.tile([P, P], BF16, name="bank")
         nc.tensor.transpose(out=gamma_ps[:], in_=gamma_rows[:], identity=ident_bf[:])
 
-        grad_t, grad_gamma_t, grad_gamma = {}, {}, {}
+        def cols_of(b):
+            return slice(b * P, (b + 1) * P)
+
+        def half_of(n):
+            return slice(n * N_TILE, (n + 1) * N_TILE)
 
         def square(k):
             for g in (2 * k, 2 * k + 1):
                 nc.scalar.activation(out=u_to_r[:, g, :], in_=u_to_r[:, g, :], func=ACT.Square, bias=-0.5, scale=1.0)
 
-        def turn(k, n):
-            grad_t[k, n] = banks.tile([P, 4, 2, P], BF16, name="bank")
-            for b in range(4):
-                for i in range(2):
-                    first = (4 * n + b) * P
-                    nc.tensor.transpose(
-                        out=grad_t[k, n][:, b, i, :], in_=grad_sb[:, 2 * k + i, first : first + P], identity=ident_bf[:]
-                    )
+        def turn(matrix_sb, groups, blocks):
+            turned_ps = banks.tile([P, len(blocks), len(groups), P], BF16, name="bank")
+            for j, b in enumerate(blocks):
+                for i, g in enumerate(groups):
+                    nc.tensor.transpose(out=turned_ps[:, j, i, :], in_=matrix_sb[:, g, cols_of(b)], identity=ident_bf[:])
+            return turned_ps
 
-        def times_gamma(k, n):
-            grad_gamma_t[k, n] = turned.tile([P, 4, 2, P], F32, name="grad_gamma_t")
-            for b in range(4):
+        def scale(turned_ps, groups, blocks, factor):
+            scaled = turned.tile([P, len(blocks), len(groups), P], F32, name="scaled")
+            for j, b in enumerate(blocks):
                 nc.scalar.activation(
-                    out=grad_gamma_t[k, n][:, b, :, :], in_=grad_t[k, n][:, b, :, :], func=ACT.Copy,
-                    scale=gamma_col[:, 4 * n + b : 4 * n + b + 1],
+                    out=scaled[:, j, :, :], in_=turned_ps[:, j, :, :], func=ACT.Copy, scale=factor[:, b : b + 1]
                 )
+            return scaled
 
-        def turn_back(k, n):
-            for i in range(2):
-                grad_gamma[2 * k + i, n] = banks.tile([P, N_TILE], F32, name="bank")
-                for b in range(4):
-                    nc.tensor.transpose(
-                        out=grad_gamma[2 * k + i, n][:, b * P : (b + 1) * P], in_=grad_gamma_t[k, n][:, b, i, :],
-                        identity=ident_f32[:],
-                    )
+        def turn_back(parts, groups, blocks, into):
+            for i, g in enumerate(groups):
+                for first in range(0, len(blocks), 4):
+                    bank = banks.tile([P, N_TILE], F32, name="bank")
+                    into[g, blocks[first] // 4] = bank
+                    for j in range(first, first + 4):
+                        for a, part in enumerate(parts):
+                            nc.tensor.matmul(
+                                out=bank[:, cols_of(j - first)], lhsT=part[:, j, i, :], rhs=ident_f32[:], is_transpose=True,
+                                start=(a == 0), stop=(a == len(parts) - 1),
+                            )
 
-        diff, diff_ps = {}, {}
+        diff, factor_ps, grad_gamma = {}, {}, {}
+        ALL_BLOCKS = tuple(range(BLOCKS))
+        ON_VECTOR = (0, 1)
+        ON_TENSOR = (2, 4, 6)
+        THROUGH_SCALAR = (3, 5, 7)
 
-        def subtract(g):
+        def subtract_on_vector(g):
             diff[g] = scratch.tile([P, COLS], F32, name="diff")
             nc.vector.tensor_tensor(out=diff[g][:], in0=h_sb[:, g, :], in1=c_sb[:, g, :], op=ALU.subtract)
 
         def subtract_on_tensor(g):
             for n in range(HALVES):
-                half = slice(n * N_TILE, (n + 1) * N_TILE)
-                diff_ps[g, n] = banks.tile([P, N_TILE], F32, name="bank")
-                nc.tensor.matmul(out=diff_ps[g, n][:], lhsT=ident_bf[:], rhs=h_sb[:, g, half], start=True, stop=False)
-                nc.tensor.matmul(out=diff_ps[g, n][:], lhsT=ident_neg[:], rhs=c_sb[:, g, half], start=False, stop=True)
+                factor_ps[g, n] = banks.tile([P, N_TILE], F32, name="bank")
+                nc.tensor.matmul(out=factor_ps[g, n][:], lhsT=ident_bf[:], rhs=h_sb[:, g, half_of(n)], start=True, stop=False)
+                nc.tensor.matmul(out=factor_ps[g, n][:], lhsT=ident_neg[:], rhs=c_sb[:, g, half_of(n)], start=False, stop=True)
+
+        def pair(k, kind):
+            return tuple(g for g in (2 * k, 2 * k + 1) if g in kind) if k < 4 else ()
+
+        def chunks(groups):
+            count = BLOCKS // len(groups)
+            return [ALL_BLOCKS[first : first + count] for first in range(0, BLOCKS, count)]
 
         def times_gate(g):
             if g in diff:
@@ -169,18 +190,21 @@ def tile_layernormgrucell_pb_v_kernel(
                 )
             else:
                 for n in range(HALVES):
-                    half = slice(n * N_TILE, (n + 1) * N_TILE)
                     nc.vector.scalar_tensor_tensor(
-                        out=u_to_r[:, g, half], in0=u_to_r[:, g, half], scalar=0.25, in1=diff_ps[g, n][:],
+                        out=u_to_r[:, g, half_of(n)], in0=u_to_r[:, g, half_of(n)], scalar=0.25, in1=factor_ps[g, n][:],
                         op0=ALU.subtract, op1=ALU.mult,
                     )
 
-        def times_grad(k):
-            for n in range(HALVES):
-                half = slice(n * N_TILE, (n + 1) * N_TILE)
-                for g in (2 * k, 2 * k + 1):
+        def times_grad(g):
+            if g in THROUGH_SCALAR:
+                nc.vector.scalar_tensor_tensor(
+                    out=u_to_r[:, g, :], in0=u_to_r[:, g, :], scalar=rstd_sb[:, g : g + 1],
+                    in1=grad_sb[:, g, :], op0=ALU.mult, op1=ALU.mult, accum_out=sum_r_half[:, g, 0:1],
+                )
+            else:
+                for n in range(HALVES):
                     nc.vector.scalar_tensor_tensor(
-                        out=u_to_r[:, g, half], in0=u_to_r[:, g, half], scalar=rstd_sb[:, g : g + 1],
+                        out=u_to_r[:, g, half_of(n)], in0=u_to_r[:, g, half_of(n)], scalar=rstd_sb[:, g : g + 1],
                         in1=grad_gamma[g, n][:], op0=ALU.mult, op1=ALU.mult, accum_out=sum_r_half[:, g, n : n + 1],
                     )
 
@@ -195,19 +219,23 @@ def tile_layernormgrucell_pb_v_kernel(
             nc.vector.tensor_reduce(out=sum_r[:, both], in_=sum_r_half[:, both, :], axis=mybir.AxisListType.X, op=ALU.add)
             nc.vector.tensor_scalar(out=mean_r[:, both], in0=sum_r[:, both], scalar1=1.0 / COLS, scalar2=None, op0=ALU.mult)
 
-        def make_shift(k):
-            for g in (2 * k, 2 * k + 1):
-                nc.scalar.activation(
-                    out=xn_to_shift[:, g, :], in_=xn_to_shift[:, g, :], func=ACT.Identity,
-                    scale=mean_r_xn[:, g : g + 1], bias=mean_r[:, g : g + 1],
-                )
+        def shift_on_gpsimd(g):
+            nc.gpsimd.tensor_scalar(
+                out=xn_to_shift[:, g, :], in0=xn_to_shift[:, g, :],
+                scalar1=mean_r_xn[:, g : g + 1], scalar2=mean_r[:, g : g + 1], op0=ALU.mult, op1=ALU.add,
+            )
+
+        def shift_on_scalar(g, cols):
+            nc.scalar.activation(
+                out=xn_to_shift[:, g, cols], in_=xn_to_shift[:, g, cols], func=ACT.Identity,
+                scale=mean_r_xn[:, g : g + 1], bias=mean_r[:, g : g + 1],
+            )
 
         def regroup_x(s, n, on_scalar):
-            half = slice(n * N_TILE, (n + 1) * N_TILE)
             copy = nc.scalar.copy if on_scalar else nc.vector.tensor_copy
             copy(
-                out=grouped_in_runs(x_grouped[:, s, half, :]),
-                in_=rows_in_runs(x_sb[:, s * PACK : (s + 1) * PACK, half]),
+                out=grouped_in_runs(x_grouped[:, s, half_of(n), :]),
+                in_=rows_in_runs(x_sb[:, s * PACK : (s + 1) * PACK, half_of(n)]),
             )
 
         def quantise_x(s):
@@ -219,45 +247,33 @@ def tile_layernormgrucell_pb_v_kernel(
 
         dv_grouped, acc = {}, {}
 
-        def late_shift(m):
-            dv_cols = slice(m * M_TILE, (m + 1) * M_TILE)
-            for g in (6, 7):
-                nc.vector.tensor_scalar(
-                    out=xn_to_shift[:, g, dv_cols], in0=xn_to_shift[:, g, dv_cols],
-                    scalar1=mean_r_xn[:, g : g + 1], scalar2=mean_r[:, g : g + 1], op0=ALU.mult, op1=ALU.add,
-                )
-
         def finish_dv(m, s):
-            dv_cols = slice(m * M_TILE, (m + 1) * M_TILE)
             groups = slice(s * PACK, (s + 1) * PACK)
             dv_grouped[m, s] = block.tile([P, M_TILE, PACK], BF16, name="dv_grouped", align_bytes=64)
             nc.vector.tensor_tensor(
                 out=grouped_in_runs(dv_grouped[m, s][:]),
-                in0=rows_in_runs(u_to_r[:, groups, dv_cols]),
-                in1=rows_in_runs(xn_to_shift[:, groups, dv_cols]),
+                in0=rows_in_runs(u_to_r[:, groups, cols_of(m)]),
+                in1=rows_in_runs(xn_to_shift[:, groups, cols_of(m)]),
                 op=ALU.subtract,
             )
 
         def quantise_dv(m, s):
-            dv_cols = slice(m * M_TILE, (m + 1) * M_TILE)
             nc.vector.quantize_mx(
-                out=dv_codes[:, s, dv_cols].bitcast(E5M2_X4),
-                scales=dv_scales[:, s, dv_cols],
+                out=dv_codes[:, s, cols_of(m)].bitcast(E5M2_X4),
+                scales=dv_scales[:, s, cols_of(m)],
                 in_=dv_grouped[m, s][:].rearrange("p w j -> p (w j)"),
             )
 
         def multiply(m, s):
-            dv_cols = slice(m * M_TILE, (m + 1) * M_TILE)
             for n in range(HALVES):
-                half = slice(n * N_TILE, (n + 1) * N_TILE)
                 if s == 0:
                     acc[m, n] = banks.tile([P, N_TILE], F32, name="bank")
                 nc.tensor.matmul_mx(
                     out=acc[m, n][:],
-                    lhsT=dv_codes[:, s, dv_cols].bitcast(E5M2_X4),
-                    lhsT_scale=dv_scales[:, s, dv_cols],
-                    rhs=x_codes[:, s, half].bitcast(E4M3_X4),
-                    rhs_scale=x_scales[:, s, half],
+                    lhsT=dv_codes[:, s, cols_of(m)].bitcast(E5M2_X4),
+                    lhsT_scale=dv_scales[:, s, cols_of(m)],
+                    rhs=x_codes[:, s, half_of(n)].bitcast(E4M3_X4),
+                    rhs_scale=x_scales[:, s, half_of(n)],
                     start=(s == 0),
                     stop=(s == PASSES - 1),
                 )
@@ -266,29 +282,33 @@ def tile_layernormgrucell_pb_v_kernel(
             for n in range(HALVES):
                 out_sb = result.tile([P, N_TILE], F32, name="out_sb")
                 nc.scalar.copy(out=out_sb[:], in_=acc[m, n][:])
-                nc.sync.dma_start(
-                    out=out[m * M_TILE : (m + 1) * M_TILE, n * N_TILE : (n + 1) * N_TILE], in_=out_sb[:]
-                )
+                nc.sync.dma_start(out=out[cols_of(m), half_of(n)], in_=out_sb[:])
 
-        ON_TENSOR = (4, 5, 6)
+        ahead_blocks = min(EARLY_2 + EARLY_3, 4)
+        products = [(m, 0) for m in range(ahead_blocks)] + [(m, 1) for m in range(ahead_blocks)]
+        products += [(m, s) for m in range(ahead_blocks, BLOCKS) for s in range(PASSES)]
+        quantised = []
 
-        def start_pair(k):
-            for g in (2 * k, 2 * k + 1):
-                if g in ON_TENSOR:
-                    subtract_on_tensor(g)
-                else:
-                    subtract(g)
+        def make_dv(units, may_multiply):
+            finish_dv(units[0][0], units[0][1])
+            for i, unit in enumerate(units):
+                if i + 1 < len(units):
+                    finish_dv(units[i + 1][0], units[i + 1][1])
+                quantise_dv(unit[0], unit[1])
+                quantised.append(unit)
+                while may_multiply and products and products[0] in quantised:
+                    m, s = products[0]
+                    products.remove(products[0])
+                    multiply(m, s)
+                    if s == 1:
+                        store(m)
 
-        def gates(k):
-            for g in (2 * k, 2 * k + 1):
-                times_gate(g)
+        EARLY = (EARLY_2, EARLY_3)
 
-        def early_dv(blocks):
-            finish_dv(blocks[0], 0)
-            for i, m in enumerate(blocks):
-                if i + 1 < len(blocks):
-                    finish_dv(blocks[i + 1], 0)
-                quantise_dv(m, 0)
+        def E_ORDER(k):
+            return (2 * k, 2 * k + 1)
+
+        first_pass = [(m, 0) for m in range(BLOCKS)]
 
         regroup_x(0, 0, False)
         regroup_x(0, 1, False)
@@ -296,41 +316,43 @@ def tile_layernormgrucell_pb_v_kernel(
         regroup_x(1, 1, False)
         quantise_x(0)
         quantise_x(1)
-        square(0)
-        nc.scalar.copy(out=gamma_col[:], in_=gamma_ps[:, 0:BLOCKS])
-        start_pair(0)
-        turn(0, 0)
-        turn(0, 1)
-        gates(0)
+        for g in pair(0, ON_VECTOR):
+            subtract_on_vector(g)
         for k in range(4):
-            for n in range(HALVES):
-                times_gamma(k, n)
-                turn_back(k, n)
-            if k >= 1:
-                make_shift(k - 1)
-            if k + 1 < 4:
-                start_pair(k + 1)
-                square(k + 1)
-                turn(k + 1, 0)
-                turn(k + 1, 1)
-            times_grad(k)
+            square(k)
+            if k == 0:
+                nc.scalar.copy(out=gamma_col[:], in_=gamma_ps[:, 0:BLOCKS])
+                nc.scalar.mul(out=gamma_neg[:], in_=gamma_ps[:, 0:BLOCKS], mul=-1.0)
+            with_grad = tuple(g for g in (2 * k, 2 * k + 1) if g not in THROUGH_SCALAR)
+            grad_t = [turn(grad_sb, with_grad, blocks) for blocks in chunks(with_grad)]
+            ahead = pair(k + 1, THROUGH_SCALAR)
+            h_t = [turn(h_sb, (g,), ALL_BLOCKS) for g in ahead]
+            c_t = [turn(c_sb, (g,), ALL_BLOCKS) for g in ahead]
+            for i, blocks in enumerate(chunks(with_grad)):
+                grad_gamma_t = scale(grad_t[i], with_grad, blocks, gamma_col)
+                turn_back((grad_gamma_t,), with_grad, blocks, grad_gamma)
+            for g in pair(k + 1, ON_TENSOR):
+                subtract_on_tensor(g)
+            for i, g in enumerate(ahead):
+                h_gamma_t = scale(h_t[i], (g,), ALL_BLOCKS, gamma_col)
+                c_gamma_t = scale(c_t[i], (g,), ALL_BLOCKS, gamma_neg)
+                turn_back((h_gamma_t, c_gamma_t), (g,), ALL_BLOCKS, factor_ps)
+            for g in (2 * k, 2 * k + 1):
+                times_gate(g)
+            for g in E_ORDER(k):
+                times_grad(g)
+            if k >= 2 and EARLY[k - 2]:
+                make_dv(first_pass[: EARLY[k - 2]], False)
+                first_pass = first_pass[EARLY[k - 2] :]
             means(k)
-            if k == 2:
-                early_dv((0, 1, 2, 3))
-            if k + 1 < 4:
-                gates(k + 1)
-        for m in range(4):
-            multiply(m, 0)
-        units = [(m, 1) for m in range(4)] + [(m, s) for m in range(4, BLOCKS) for s in range(PASSES)]
-        late_shift(0)
-        late_shift(1)
-        finish_dv(0, 1)
-        for i, (m, s) in enumerate(units):
-            if s == 1 and m + 2 < BLOCKS:
-                late_shift(m + 2)
-            if i + 1 < len(units):
-                finish_dv(units[i + 1][0], units[i + 1][1])
-            quantise_dv(m, s)
-            multiply(m, s)
-            if s == 1:
-                store(m)
+            if k < 3:
+                for g in (2 * k, 2 * k + 1):
+                    if SHIFT_G:
+                        shift_on_gpsimd(g)
+                    else:
+                        shift_on_scalar(g, slice(0, COLS))
+        for cols in (slice(0, 256), slice(256, 512), slice(512, COLS)):
+            shift_on_scalar(6, cols)
+            shift_on_scalar(7, cols)
+        fill = first_pass[:FILL]
+        make_dv(fill + [unit for unit in products if unit not in quantised and unit not in fill], True)

@@ -22,13 +22,15 @@ N_TILE = 512
 BLOCKS = COLS // M_TILE
 HALVES = COLS // N_TILE
 RUN = 4
-EARLY_2 = 0
-EARLY_3 = 0
-SHIFT_G = True
+ON_VECTOR = (0, 1)
+ON_TENSOR = (2, 4, 6)
+THROUGH_SCALAR = (3, 5, 7)
+S_FIRST = True
+SMALL_AFTER = 1
+LAST_SPLIT = 0
+LAST_ON_SCALAR = False
+EARLY = 1
 FILL = 2
-
-FLOPS = 2 * ROWS * COLS * COLS
-BYTES = 4 * ROWS * COLS * 2 + 3 * ROWS * COLS * 4 + COLS * 2 + ROWS * 4
 
 
 def by_group(matrix):
@@ -47,6 +49,17 @@ def tile_layernormgrucell_pb_v_kernel(
     tc, x, h, c, W_u, U_u, ln_gamma, ln_beta, u, xn, rstd, grad_out, out
 ):
     nc = tc.nc
+    loads = [("x", 0, 4), ("h", 0, 2), ("c", 0, 2), ("u", 0, 2), ("g", 0, 2)]
+    for k in range(1, 4):
+        loads += [("h", 2 * k, 2), ("c", 2 * k, 2), ("n", 2 * k - 2, 2), ("u", 2 * k, 2), ("g", 2 * k, 2)]
+    loads += [("x", 4, 4), ("n", 6, 2)]
+    plan = {
+        (0, "A0"): [("rx", 0, 0, False), ("rx", 0, 1, True)],
+        (0, "a"): [("b", 0), ("b", 1), ("qx", 0)],
+        (3, "A1"): [("rx", 1, 0, True), ("rx", 1, 1, True)],
+        (3, "a"): [("units", 1)],
+        (4, "a"): [("qx", 1)],
+    }
     with (
         tc.manual_schedule(),
         tc.tile_pool(name="resident", bufs=1) as resident,
@@ -81,11 +94,6 @@ def tile_layernormgrucell_pb_v_kernel(
         ident_neg = resident.tile([P, P], BF16)
 
         nc.vector.memset(gamma_rows[:].bitcast(I32), 0)
-        nc.scalar.dma_start(out=gamma_rows[0:BLOCKS, :], in_=ln_gamma[1:2, :].rearrange("o (b p) -> (o b) p", p=P))
-        nc.scalar.dma_start(
-            out=rstd_sb[:].rearrange("p (s j) -> p s j", j=PACK),
-            in_=rstd.rearrange("(s p j) o -> p s (j o)", s=PASSES, p=P, j=PACK),
-        )
         nc.vector.memset(warm[:], 0.0)
         nc.vector.memset(sum_r_half[:], 0.0)
         nc.scalar.activation(out=warm[:, 1:2], in_=warm[:, 0:1], func=ACT.Square)
@@ -97,27 +105,15 @@ def tile_layernormgrucell_pb_v_kernel(
             s, j = first // PACK, first % PACK
             nc.sync.dma_start(out=tile_sb[:, first : first + count, :], in_=by_group(matrix)[:, s, j : j + count, :])
 
-        def load_h_c(k):
-            load(h_sb, h, 2 * k, 2)
-            load(c_sb, c, 2 * k, 2)
-
-        def load_both(tile_sb, matrix, k):
-            load(tile_sb, matrix, 2 * k, 2)
-
-        def load_x(s):
-            load(x_sb, x, s * PACK, PACK)
-
-        load_x(0)
-        load_x(1)
-        load_h_c(0)
-        load_both(u_to_r, u, 0)
-        load_both(grad_sb, grad_out, 0)
-        for k in range(1, 4):
-            load_h_c(k)
-            load_both(xn_to_shift, xn, k - 1)
-            load_both(u_to_r, u, k)
-            load_both(grad_sb, grad_out, k)
-        load_both(xn_to_shift, xn, 3)
+        sources = {"x": (x_sb, x), "h": (h_sb, h), "c": (c_sb, c), "u": (u_to_r, u), "g": (grad_sb, grad_out), "n": (xn_to_shift, xn)}
+        for i, (name, first, count) in enumerate(loads):
+            if i == SMALL_AFTER:
+                nc.sync.dma_start(out=gamma_rows[0:BLOCKS, :], in_=ln_gamma[1:2, :].rearrange("o (b p) -> (o b) p", p=P))
+                nc.sync.dma_start(
+                    out=rstd_sb[:].rearrange("p (s j) -> p s j", j=PACK),
+                    in_=rstd.rearrange("(s p j) o -> p s (j o)", s=PASSES, p=P, j=PACK),
+                )
+            load(sources[name][0], sources[name][1], first, count)
 
         gamma_ps = banks.tile([P, P], BF16, name="bank")
         nc.tensor.transpose(out=gamma_ps[:], in_=gamma_rows[:], identity=ident_bf[:])
@@ -161,9 +157,6 @@ def tile_layernormgrucell_pb_v_kernel(
 
         diff, factor_ps, grad_gamma = {}, {}, {}
         ALL_BLOCKS = tuple(range(BLOCKS))
-        ON_VECTOR = (0, 1)
-        ON_TENSOR = (2, 4, 6)
-        THROUGH_SCALAR = (3, 5, 7)
 
         def subtract_on_vector(g):
             diff[g] = scratch.tile([P, COLS], F32, name="diff")
@@ -195,14 +188,14 @@ def tile_layernormgrucell_pb_v_kernel(
                         op0=ALU.subtract, op1=ALU.mult,
                     )
 
-        def times_grad(g):
+        def times_grad(g, halves):
             if g in THROUGH_SCALAR:
                 nc.vector.scalar_tensor_tensor(
                     out=u_to_r[:, g, :], in0=u_to_r[:, g, :], scalar=rstd_sb[:, g : g + 1],
                     in1=grad_sb[:, g, :], op0=ALU.mult, op1=ALU.mult, accum_out=sum_r_half[:, g, 0:1],
                 )
             else:
-                for n in range(HALVES):
+                for n in halves:
                     nc.vector.scalar_tensor_tensor(
                         out=u_to_r[:, g, half_of(n)], in0=u_to_r[:, g, half_of(n)], scalar=rstd_sb[:, g : g + 1],
                         in1=grad_gamma[g, n][:], op0=ALU.mult, op1=ALU.mult, accum_out=sum_r_half[:, g, n : n + 1],
@@ -281,10 +274,16 @@ def tile_layernormgrucell_pb_v_kernel(
         def store(m):
             for n in range(HALVES):
                 out_sb = result.tile([P, N_TILE], F32, name="out_sb")
-                nc.scalar.copy(out=out_sb[:], in_=acc[m, n][:])
-                nc.sync.dma_start(out=out[cols_of(m), half_of(n)], in_=out_sb[:])
+                if m >= BLOCKS - LAST_SPLIT and n == 0:
+                    nc.vector.tensor_copy(out=out_sb[:], in_=acc[m, n][:])
+                else:
+                    nc.scalar.copy(out=out_sb[:], in_=acc[m, n][:])
+                if m == BLOCKS - 1 and n == 1 and LAST_ON_SCALAR:
+                    nc.scalar.dma_start(out=out[cols_of(m), half_of(n)], in_=out_sb[:])
+                else:
+                    nc.sync.dma_start(out=out[cols_of(m), half_of(n)], in_=out_sb[:])
 
-        ahead_blocks = min(EARLY_2 + EARLY_3, 4)
+        ahead_blocks = min(EARLY, 4)
         products = [(m, 0) for m in range(ahead_blocks)] + [(m, 1) for m in range(ahead_blocks)]
         products += [(m, s) for m in range(ahead_blocks, BLOCKS) for s in range(PASSES)]
         quantised = []
@@ -303,56 +302,68 @@ def tile_layernormgrucell_pb_v_kernel(
                     if s == 1:
                         store(m)
 
-        EARLY = (EARLY_2, EARLY_3)
-
-        def E_ORDER(k):
-            return (2 * k, 2 * k + 1)
-
         first_pass = [(m, 0) for m in range(BLOCKS)]
 
-        regroup_x(0, 0, False)
-        regroup_x(0, 1, False)
-        regroup_x(1, 0, True)
-        regroup_x(1, 1, False)
-        quantise_x(0)
-        quantise_x(1)
-        for g in pair(0, ON_VECTOR):
-            subtract_on_vector(g)
+        def extra(tokens):
+            for token in tokens:
+                if token[0] == "rx":
+                    regroup_x(token[1], token[2], token[3])
+                elif token[0] == "qx":
+                    quantise_x(token[1])
+                elif token[0] == "b":
+                    subtract_on_vector(token[1])
+                elif token[0] == "units":
+                    make_dv(first_pass[: token[1]], False)
+                    for unit in first_pass[: token[1]]:
+                        first_pass.remove(unit)
+
         for k in range(4):
+            extra(plan.get((k, "A0"), ()))
             square(k)
             if k == 0:
                 nc.scalar.copy(out=gamma_col[:], in_=gamma_ps[:, 0:BLOCKS])
                 nc.scalar.mul(out=gamma_neg[:], in_=gamma_ps[:, 0:BLOCKS], mul=-1.0)
             with_grad = tuple(g for g in (2 * k, 2 * k + 1) if g not in THROUGH_SCALAR)
-            grad_t = [turn(grad_sb, with_grad, blocks) for blocks in chunks(with_grad)]
+            grad_t = [turn(grad_sb, with_grad, blocks) for blocks in chunks(with_grad)] if with_grad else []
             ahead = pair(k + 1, THROUGH_SCALAR)
             h_t = [turn(h_sb, (g,), ALL_BLOCKS) for g in ahead]
             c_t = [turn(c_sb, (g,), ALL_BLOCKS) for g in ahead]
-            for i, blocks in enumerate(chunks(with_grad)):
+            for i in range(len(grad_t)):
+                blocks = chunks(with_grad)[i]
                 grad_gamma_t = scale(grad_t[i], with_grad, blocks, gamma_col)
                 turn_back((grad_gamma_t,), with_grad, blocks, grad_gamma)
+            extra(plan.get((k, "A1"), ()))
             for g in pair(k + 1, ON_TENSOR):
                 subtract_on_tensor(g)
             for i, g in enumerate(ahead):
                 h_gamma_t = scale(h_t[i], (g,), ALL_BLOCKS, gamma_col)
                 c_gamma_t = scale(c_t[i], (g,), ALL_BLOCKS, gamma_neg)
                 turn_back((h_gamma_t, c_gamma_t), (g,), ALL_BLOCKS, factor_ps)
+            extra(plan.get((k, "A2"), ()))
+            extra(plan.get((k, "a"), ()))
             for g in (2 * k, 2 * k + 1):
                 times_gate(g)
-            for g in E_ORDER(k):
-                times_grad(g)
-            if k >= 2 and EARLY[k - 2]:
-                make_dv(first_pass[: EARLY[k - 2]], False)
-                first_pass = first_pass[EARLY[k - 2] :]
+            extra(plan.get((k, "b"), ()))
+            if len(with_grad) == 2:
+                for n in range(HALVES):
+                    for g in with_grad:
+                        times_grad(g, (n,))
+            else:
+                for i, g in enumerate(sorted((2 * k, 2 * k + 1), key=lambda g: (g in THROUGH_SCALAR) != S_FIRST)):
+                    if i == 1:
+                        extra(plan.get((k, "b2"), ()))
+                    times_grad(g, (0, 1))
+            extra(plan.get((k, "c"), ()))
             means(k)
             if k < 3:
-                for g in (2 * k, 2 * k + 1):
-                    if SHIFT_G:
-                        shift_on_gpsimd(g)
-                    else:
-                        shift_on_scalar(g, slice(0, COLS))
+                shift_on_gpsimd(2 * k)
+                shift_on_gpsimd(2 * k + 1)
+            extra(plan.get((k, "d"), ()))
         for cols in (slice(0, 256), slice(256, 512), slice(512, COLS)):
             shift_on_scalar(6, cols)
             shift_on_scalar(7, cols)
         fill = first_pass[:FILL]
-        make_dv(fill + [unit for unit in products if unit not in quantised and unit not in fill], True)
+        if fill:
+            make_dv(fill, False)
+        extra(plan.get((4, "a"), ()))
+        make_dv([unit for unit in products if unit not in quantised], True)

@@ -49,17 +49,8 @@ def tile_layernormgrucell_pb_v_kernel(
     tc, x, h, c, W_u, U_u, ln_gamma, ln_beta, u, xn, rstd, grad_out, out
 ):
     nc = tc.nc
-    loads = [("x", 0, 4), ("h", 0, 2), ("c", 0, 2), ("u", 0, 2), ("g", 0, 2)]
-    for k in range(1, 4):
-        loads += [("h", 2 * k, 2), ("c", 2 * k, 2), ("n", 2 * k - 2, 2), ("u", 2 * k, 2), ("g", 2 * k, 2)]
-    loads += [("x", 4, 4), ("n", 6, 2)]
-    plan = {
-        (0, "A0"): [("rx", 0, 0, False), ("rx", 0, 1, True)],
-        (0, "a"): [("b", 0), ("b", 1), ("qx", 0)],
-        (3, "A1"): [("rx", 1, 0, True), ("rx", 1, 1, True)],
-        (3, "a"): [("units", 1)],
-        (4, "a"): [("qx", 1)],
-    }
+    loads = [("x",0,4),("h",0,2),("c",0,2),("u",0,2),("g",0,2),("h",2,2),("c",2,2),("n",0,2),("u",2,2),("g",2,2),("h",4,2),("c",4,2),("n",2,2),("u",4,2),("g",4,2),("h",6,2),("c",6,2),("n",4,2),("u",6,2),("g",6,2),("x",4,4),("n",6,2)]
+    plan = {(0,"A0"):[("rx",0,0,False),("rx",0,1,True)],(0,"a"):[("b",0),("b",1),("qx",0)],(3,"A1"):[("rx",1,0,True),("rx",1,1,True)],(4,"a"):[("qx",1)],(3,"a"):[("fin",0)],(3,"b"):[("qdv",0)]}
     with (
         tc.manual_schedule(),
         tc.tile_pool(name="resident", bufs=1) as resident,
@@ -125,7 +116,7 @@ def tile_layernormgrucell_pb_v_kernel(
             return slice(n * N_TILE, (n + 1) * N_TILE)
 
         def square(k):
-            for g in (2 * k, 2 * k + 1):
+            for g in sorted((2 * k, 2 * k + 1), key=lambda g: (g in THROUGH_SCALAR) != S_FIRST):
                 nc.scalar.activation(out=u_to_r[:, g, :], in_=u_to_r[:, g, :], func=ACT.Square, bias=-0.5, scale=1.0)
 
         def turn(matrix_sb, groups, blocks):
@@ -201,15 +192,16 @@ def tile_layernormgrucell_pb_v_kernel(
                         in1=grad_gamma[g, n][:], op0=ALU.mult, op1=ALU.mult, accum_out=sum_r_half[:, g, n : n + 1],
                     )
 
-        def means(k):
-            for g in (2 * k, 2 * k + 1):
+        def means(k, order):
+            both = slice(2 * k, 2 * k + 2)
+            for i, g in enumerate(order):
                 junk = scratch.tile([P, COLS], F32, name="diff")
                 nc.vector.scalar_tensor_tensor(
                     out=junk[:], in0=u_to_r[:, g, :], scalar=1.0 / COLS, in1=xn_to_shift[:, g, :],
                     op0=ALU.mult, op1=ALU.mult, accum_out=mean_r_xn[:, g : g + 1],
                 )
-            both = slice(2 * k, 2 * k + 2)
-            nc.vector.tensor_reduce(out=sum_r[:, both], in_=sum_r_half[:, both, :], axis=mybir.AxisListType.X, op=ALU.add)
+                if i == 0:
+                    nc.vector.tensor_reduce(out=sum_r[:, both], in_=sum_r_half[:, both, :], axis=mybir.AxisListType.X, op=ALU.add)
             nc.vector.tensor_scalar(out=mean_r[:, both], in0=sum_r[:, both], scalar1=1.0 / COLS, scalar2=None, op0=ALU.mult)
 
         def shift_on_gpsimd(g):
@@ -312,6 +304,12 @@ def tile_layernormgrucell_pb_v_kernel(
                     quantise_x(token[1])
                 elif token[0] == "b":
                     subtract_on_vector(token[1])
+                elif token[0] == "fin":
+                    finish_dv(token[1], 0)
+                elif token[0] == "qdv":
+                    quantise_dv(token[1], 0)
+                    quantised.append((token[1], 0))
+                    first_pass.remove((token[1], 0))
                 elif token[0] == "units":
                     make_dv(first_pass[: token[1]], False)
                     for unit in first_pass[: token[1]]:
@@ -341,7 +339,8 @@ def tile_layernormgrucell_pb_v_kernel(
                 turn_back((h_gamma_t, c_gamma_t), (g,), ALL_BLOCKS, factor_ps)
             extra(plan.get((k, "A2"), ()))
             extra(plan.get((k, "a"), ()))
-            for g in (2 * k, 2 * k + 1):
+            order = sorted((2 * k, 2 * k + 1), key=lambda g: (g in THROUGH_SCALAR) != S_FIRST)
+            for g in order:
                 times_gate(g)
             extra(plan.get((k, "b"), ()))
             if len(with_grad) == 2:
@@ -354,7 +353,7 @@ def tile_layernormgrucell_pb_v_kernel(
                         extra(plan.get((k, "b2"), ()))
                     times_grad(g, (0, 1))
             extra(plan.get((k, "c"), ()))
-            means(k)
+            means(k, order)
             if k < 3:
                 shift_on_gpsimd(2 * k)
                 shift_on_gpsimd(2 * k + 1)

@@ -30,6 +30,7 @@ SMALL_AFTER = 1
 LAST_SPLIT = 0
 LAST_ON_SCALAR = False
 EARLY = 1
+AHEAD = 3
 FILL = 2
 
 
@@ -275,7 +276,7 @@ def tile_layernormgrucell_pb_v_kernel(
                 else:
                     nc.sync.dma_start(out=out[cols_of(m), half_of(n)], in_=out_sb[:])
 
-        ahead_blocks = min(EARLY, 4)
+        ahead_blocks = min(AHEAD, 4)
         products = [(m, 0) for m in range(ahead_blocks)] + [(m, 1) for m in range(ahead_blocks)]
         products += [(m, s) for m in range(ahead_blocks, BLOCKS) for s in range(PASSES)]
         quantised = []

@@ -31,6 +31,9 @@ LAST_SPLIT = 0
 LAST_ON_SCALAR = False
 EARLY = 1
 AHEAD = 3
+G_SHIFTS = (0, 2, 4)
+TINY_G = False
+SQ_PIECES = 1
 FILL = 2
 
 
@@ -51,13 +54,14 @@ def tile_layernormgrucell_pb_v_kernel(
 ):
     nc = tc.nc
     loads = [("x",0,4),("h",0,2),("c",0,2),("u",0,2),("g",0,2),("h",2,2),("c",2,2),("n",0,2),("u",2,2),("g",2,2),("h",4,2),("c",4,2),("n",2,2),("u",4,2),("g",4,2),("h",6,2),("c",6,2),("n",4,2),("u",6,2),("g",6,2),("x",4,4),("n",6,2)]
-    plan = {(0,"A0"):[("rx",0,0,False),("rx",0,1,True)],(0,"a"):[("b",0),("b",1),("qx",0)],(3,"A1"):[("rx",1,0,True),("rx",1,1,True)],(4,"a"):[("qx",1)],(3,"a"):[("fin",0)],(3,"b"):[("qdv",0)]}
+    plan = {(0,"A0"):[("rx",0,0,False),("rx",0,1,True)],(0,"a"):[("b",0),("b",1),("qx",0)],(3,"A1"):[("sh",5),("rx",1,0,True),("rx",1,1,True)],(4,"a"):[("qx",1)],(3,"a"):[("fin",0)],(3,"b"):[("qdv",0)],(2,"A0"):[("sh",1)],(3,"A0"):[("sh",3)]}
     with (
         tc.manual_schedule(),
         tc.tile_pool(name="resident", bufs=1) as resident,
         tc.tile_pool(name="scratch", bufs=4) as scratch,
         tc.tile_pool(name="turned", bufs=5) as turned,
         tc.tile_pool(name="block", bufs=4) as block,
+        tc.tile_pool(name="early", bufs=8) as early,
         tc.tile_pool(name="result", bufs=6) as result,
         tc.psum_pool(name="banks", bufs=8) as banks,
     ):
@@ -118,7 +122,9 @@ def tile_layernormgrucell_pb_v_kernel(
 
         def square(k):
             for g in sorted((2 * k, 2 * k + 1), key=lambda g: (g in THROUGH_SCALAR) != S_FIRST):
-                nc.scalar.activation(out=u_to_r[:, g, :], in_=u_to_r[:, g, :], func=ACT.Square, bias=-0.5, scale=1.0)
+                for n in range(SQ_PIECES):
+                    cols = slice(n * COLS // SQ_PIECES, (n + 1) * COLS // SQ_PIECES)
+                    nc.scalar.activation(out=u_to_r[:, g, cols], in_=u_to_r[:, g, cols], func=ACT.Square, bias=-0.5, scale=1.0)
 
         def turn(matrix_sb, groups, blocks):
             turned_ps = banks.tile([P, len(blocks), len(groups), P], BF16, name="bank")
@@ -201,9 +207,13 @@ def tile_layernormgrucell_pb_v_kernel(
                     out=junk[:], in0=u_to_r[:, g, :], scalar=1.0 / COLS, in1=xn_to_shift[:, g, :],
                     op0=ALU.mult, op1=ALU.mult, accum_out=mean_r_xn[:, g : g + 1],
                 )
-                if i == 0:
+                if i == 0 and not (TINY_G and k < 3):
                     nc.vector.tensor_reduce(out=sum_r[:, both], in_=sum_r_half[:, both, :], axis=mybir.AxisListType.X, op=ALU.add)
-            nc.vector.tensor_scalar(out=mean_r[:, both], in0=sum_r[:, both], scalar1=1.0 / COLS, scalar2=None, op0=ALU.mult)
+                if i == 0 and TINY_G and k < 3:
+                    nc.gpsimd.tensor_tensor(out=sum_r[:, both], in0=sum_r_half[:, both, 0], in1=sum_r_half[:, both, 1], op=ALU.add)
+                    nc.gpsimd.tensor_scalar(out=mean_r[:, both], in0=sum_r[:, both], scalar1=1.0 / COLS, scalar2=0.0, op0=ALU.mult, op1=ALU.add)
+            if not (TINY_G and k < 3):
+                nc.vector.tensor_scalar(out=mean_r[:, both], in0=sum_r[:, both], scalar1=1.0 / COLS, scalar2=None, op0=ALU.mult)
 
         def shift_on_gpsimd(g):
             nc.gpsimd.tensor_scalar(
@@ -234,12 +244,23 @@ def tile_layernormgrucell_pb_v_kernel(
         dv_grouped, acc = {}, {}
 
         def finish_dv(m, s):
+            if (m, s) in dv_grouped:
+                return
             groups = slice(s * PACK, (s + 1) * PACK)
             dv_grouped[m, s] = block.tile([P, M_TILE, PACK], BF16, name="dv_grouped", align_bytes=64)
             nc.vector.tensor_tensor(
                 out=grouped_in_runs(dv_grouped[m, s][:]),
                 in0=rows_in_runs(u_to_r[:, groups, cols_of(m)]),
                 in1=rows_in_runs(xn_to_shift[:, groups, cols_of(m)]),
+                op=ALU.subtract,
+            )
+
+        def finish_on_gpsimd(m):
+            dv_grouped[m, 0] = early.tile([P, M_TILE, PACK], BF16, name="dv_early", align_bytes=64)
+            nc.gpsimd.tensor_tensor(
+                out=dv_grouped[m, 0][:],
+                in0=u_to_r[:, 0:PACK, cols_of(m)].rearrange("p j w -> p w j"),
+                in1=xn_to_shift[:, 0:PACK, cols_of(m)].rearrange("p j w -> p w j"),
                 op=ALU.subtract,
             )
 
@@ -305,6 +326,10 @@ def tile_layernormgrucell_pb_v_kernel(
                     quantise_x(token[1])
                 elif token[0] == "b":
                     subtract_on_vector(token[1])
+                elif token[0] == "sh":
+                    shift_on_scalar(token[1], slice(0, COLS))
+                elif token[0] == "gfin":
+                    finish_on_gpsimd(token[1])
                 elif token[0] == "fin":
                     finish_dv(token[1], 0)
                 elif token[0] == "qdv":
@@ -355,9 +380,9 @@ def tile_layernormgrucell_pb_v_kernel(
                     times_grad(g, (0, 1))
             extra(plan.get((k, "c"), ()))
             means(k, order)
-            if k < 3:
-                shift_on_gpsimd(2 * k)
-                shift_on_gpsimd(2 * k + 1)
+            for g in (2 * k, 2 * k + 1):
+                if g in G_SHIFTS:
+                    shift_on_gpsimd(g)
             extra(plan.get((k, "d"), ()))
         for cols in (slice(0, 256), slice(256, 512), slice(512, COLS)):
             shift_on_scalar(6, cols)

@@ -27,8 +27,8 @@ ON_TENSOR = (2, 4, 6)
 THROUGH_SCALAR = (3, 5, 7)
 S_FIRST = True
 SMALL_AFTER = 1
-LAST_SPLIT = 0
-LAST_ON_SCALAR = False
+LAST_SPLIT = 1
+LAST_ON_SCALAR = True
 EARLY = 1
 AHEAD = 3
 G_SHIFTS = (0, 2, 4)

import concourse.mybir as mybir
from concourse.masks import make_identity

F32 = mybir.dt.float32
BF16 = mybir.dt.bfloat16
I32 = mybir.dt.int32
U32 = mybir.dt.uint32
U8 = mybir.dt.uint8
E4M3_X4 = mybir.dt.float8_e4m3fn_x4
E5M2_X4 = mybir.dt.float8_e5m2_x4
ALU = mybir.AluOpType
ACT = mybir.ActivationFunctionType

P = 128
PACK = 4
ROWS = 1024
COLS = 1024
PASSES = ROWS // (P * PACK)
GROUPS = PASSES * PACK
M_TILE = 128
N_TILE = 512
BLOCKS = COLS // M_TILE
HALVES = COLS // N_TILE
RUN = 4
ON_VECTOR = (0, 1)
ON_TENSOR = (2, 4, 6)
THROUGH_SCALAR = (3, 5, 7)
S_FIRST = True
SMALL_AFTER = 1
LAST_SPLIT = 1
LAST_ON_SCALAR = True
EARLY = 1
AHEAD = 3
G_SHIFTS = (0, 2, 4)
TINY_G = False
SQ_PIECES = 1
FILL = 2


def by_group(matrix):
    return matrix.rearrange("(s p j) w -> p s j w", s=PASSES, p=P, j=PACK)


def rows_in_runs(rows):
    return rows.rearrange("p j (q i) -> p q j i", i=RUN)


def grouped_in_runs(grouped):
    return grouped.rearrange("p (q i) j -> p q j i", i=RUN)


def tile_layernormgrucell_pb_v_kernel(
    tc, x, h, c, W_u, U_u, ln_gamma, ln_beta, u, xn, rstd, grad_out, out
):
    nc = tc.nc
    loads = [("x",0,4),("h",0,2),("c",0,2),("u",0,2),("g",0,2),("h",2,2),("c",2,2),("n",0,2),("u",2,2),("g",2,2),("h",4,2),("c",4,2),("n",2,2),("u",4,2),("g",4,2),("h",6,2),("c",6,2),("n",4,2),("u",6,2),("g",6,2),("x",4,4),("n",6,2)]
    plan = {(0,"A0"):[("rx",0,0,False),("rx",0,1,True)],(0,"a"):[("b",0),("b",1),("qx",0)],(3,"A1"):[("sh",5),("rx",1,0,True),("rx",1,1,True)],(4,"a"):[("qx",1)],(3,"a"):[("fin",0)],(3,"b"):[("qdv",0)],(2,"A0"):[("sh",1)],(3,"A0"):[("sh",3)]}
    with (
        tc.manual_schedule(),
        tc.tile_pool(name="resident", bufs=1) as resident,
        tc.tile_pool(name="scratch", bufs=4) as scratch,
        tc.tile_pool(name="turned", bufs=5) as turned,
        tc.tile_pool(name="block", bufs=4) as block,
        tc.tile_pool(name="early", bufs=8) as early,
        tc.tile_pool(name="result", bufs=6) as result,
        tc.psum_pool(name="banks", bufs=8) as banks,
    ):
        u_to_r = resident.tile([P, GROUPS, COLS], F32)
        xn_to_shift = resident.tile([P, GROUPS, COLS], F32)
        h_sb = resident.tile([P, GROUPS, COLS], BF16)
        c_sb = resident.tile([P, GROUPS, COLS], BF16)
        grad_sb = resident.tile([P, GROUPS, COLS], BF16)
        x_sb = resident.tile([P, GROUPS, COLS], BF16)
        x_grouped = resident.tile([P, PASSES, COLS, PACK], BF16, align_bytes=64)
        x_codes = resident.tile([P, PASSES, COLS], U32, align_bytes=64)
        x_scales = resident.tile([P, PASSES, COLS], U8, align_bytes=64)
        dv_codes = resident.tile([P, PASSES, COLS], U32, align_bytes=64)
        dv_scales = resident.tile([P, PASSES, COLS], U8, align_bytes=64)
        rstd_sb = resident.tile([P, GROUPS], F32)
        sum_r_half = resident.tile([P, GROUPS, HALVES], F32)
        sum_r = resident.tile([P, GROUPS], F32)
        mean_r = resident.tile([P, GROUPS], F32)
        mean_r_xn = resident.tile([P, GROUPS], F32)
        gamma_rows = resident.tile([P, P], BF16)
        gamma_col = resident.tile([P, BLOCKS], F32)
        gamma_neg = resident.tile([P, BLOCKS], F32)
        ident_bf = resident.tile([P, P], BF16)
        ident_f32 = resident.tile([P, P], F32)
        warm = resident.tile([P, 2], F32)
        ident_neg = resident.tile([P, P], BF16)

        nc.vector.memset(gamma_rows[:].bitcast(I32), 0)
        nc.vector.memset(warm[:], 0.0)
        nc.vector.memset(sum_r_half[:], 0.0)
        nc.scalar.activation(out=warm[:, 1:2], in_=warm[:, 0:1], func=ACT.Square)
        make_identity(nc, ident_bf[:])
        make_identity(nc, ident_f32[:])
        nc.scalar.mul(out=ident_neg[:], in_=ident_bf[:], mul=-1.0)

        def load(tile_sb, matrix, first, count):
            s, j = first // PACK, first % PACK
            nc.sync.dma_start(out=tile_sb[:, first : first + count, :], in_=by_group(matrix)[:, s, j : j + count, :])

        sources = {"x": (x_sb, x), "h": (h_sb, h), "c": (c_sb, c), "u": (u_to_r, u), "g": (grad_sb, grad_out), "n": (xn_to_shift, xn)}
        for i, (name, first, count) in enumerate(loads):
            if i == SMALL_AFTER:
                nc.sync.dma_start(out=gamma_rows[0:BLOCKS, :], in_=ln_gamma[1:2, :].rearrange("o (b p) -> (o b) p", p=P))
                nc.sync.dma_start(
                    out=rstd_sb[:].rearrange("p (s j) -> p s j", j=PACK),
                    in_=rstd.rearrange("(s p j) o -> p s (j o)", s=PASSES, p=P, j=PACK),
                )
            load(sources[name][0], sources[name][1], first, count)

        gamma_ps = banks.tile([P, P], BF16, name="bank")
        nc.tensor.transpose(out=gamma_ps[:], in_=gamma_rows[:], identity=ident_bf[:])

        def cols_of(b):
            return slice(b * P, (b + 1) * P)

        def half_of(n):
            return slice(n * N_TILE, (n + 1) * N_TILE)

        def square(k):
            for g in sorted((2 * k, 2 * k + 1), key=lambda g: (g in THROUGH_SCALAR) != S_FIRST):
                for n in range(SQ_PIECES):
                    cols = slice(n * COLS // SQ_PIECES, (n + 1) * COLS // SQ_PIECES)
                    nc.scalar.activation(out=u_to_r[:, g, cols], in_=u_to_r[:, g, cols], func=ACT.Square, bias=-0.5, scale=1.0)

        def turn(matrix_sb, groups, blocks):
            turned_ps = banks.tile([P, len(blocks), len(groups), P], BF16, name="bank")
            for j, b in enumerate(blocks):
                for i, g in enumerate(groups):
                    nc.tensor.transpose(out=turned_ps[:, j, i, :], in_=matrix_sb[:, g, cols_of(b)], identity=ident_bf[:])
            return turned_ps

        def scale(turned_ps, groups, blocks, factor):
            scaled = turned.tile([P, len(blocks), len(groups), P], F32, name="scaled")
            for j, b in enumerate(blocks):
                nc.scalar.activation(
                    out=scaled[:, j, :, :], in_=turned_ps[:, j, :, :], func=ACT.Copy, scale=factor[:, b : b + 1]
                )
            return scaled

        def turn_back(parts, groups, blocks, into):
            for i, g in enumerate(groups):
                for first in range(0, len(blocks), 4):
                    bank = banks.tile([P, N_TILE], F32, name="bank")
                    into[g, blocks[first] // 4] = bank
                    for j in range(first, first + 4):
                        for a, part in enumerate(parts):
                            nc.tensor.matmul(
                                out=bank[:, cols_of(j - first)], lhsT=part[:, j, i, :], rhs=ident_f32[:], is_transpose=True,
                                start=(a == 0), stop=(a == len(parts) - 1),
                            )

        diff, factor_ps, grad_gamma = {}, {}, {}
        ALL_BLOCKS = tuple(range(BLOCKS))

        def subtract_on_vector(g):
            diff[g] = scratch.tile([P, COLS], F32, name="diff")
            nc.vector.tensor_tensor(out=diff[g][:], in0=h_sb[:, g, :], in1=c_sb[:, g, :], op=ALU.subtract)

        def subtract_on_tensor(g):
            for n in range(HALVES):
                factor_ps[g, n] = banks.tile([P, N_TILE], F32, name="bank")
                nc.tensor.matmul(out=factor_ps[g, n][:], lhsT=ident_bf[:], rhs=h_sb[:, g, half_of(n)], start=True, stop=False)
                nc.tensor.matmul(out=factor_ps[g, n][:], lhsT=ident_neg[:], rhs=c_sb[:, g, half_of(n)], start=False, stop=True)

        def pair(k, kind):
            return tuple(g for g in (2 * k, 2 * k + 1) if g in kind) if k < 4 else ()

        def chunks(groups):
            count = BLOCKS // len(groups)
            return [ALL_BLOCKS[first : first + count] for first in range(0, BLOCKS, count)]

        def times_gate(g):
            if g in diff:
                nc.vector.scalar_tensor_tensor(
                    out=u_to_r[:, g, :], in0=u_to_r[:, g, :], scalar=0.25, in1=diff[g][:],
                    op0=ALU.subtract, op1=ALU.mult,
                )
            else:
                for n in range(HALVES):
                    nc.vector.scalar_tensor_tensor(
                        out=u_to_r[:, g, half_of(n)], in0=u_to_r[:, g, half_of(n)], scalar=0.25, in1=factor_ps[g, n][:],
                        op0=ALU.subtract, op1=ALU.mult,
                    )

        def times_grad(g, halves):
            if g in THROUGH_SCALAR:
                nc.vector.scalar_tensor_tensor(
                    out=u_to_r[:, g, :], in0=u_to_r[:, g, :], scalar=rstd_sb[:, g : g + 1],
                    in1=grad_sb[:, g, :], op0=ALU.mult, op1=ALU.mult, accum_out=sum_r_half[:, g, 0:1],
                )
            else:
                for n in halves:
                    nc.vector.scalar_tensor_tensor(
                        out=u_to_r[:, g, half_of(n)], in0=u_to_r[:, g, half_of(n)], scalar=rstd_sb[:, g : g + 1],
                        in1=grad_gamma[g, n][:], op0=ALU.mult, op1=ALU.mult, accum_out=sum_r_half[:, g, n : n + 1],
                    )

        def means(k, order):
            both = slice(2 * k, 2 * k + 2)
            for i, g in enumerate(order):
                junk = scratch.tile([P, COLS], F32, name="diff")
                nc.vector.scalar_tensor_tensor(
                    out=junk[:], in0=u_to_r[:, g, :], scalar=1.0 / COLS, in1=xn_to_shift[:, g, :],
                    op0=ALU.mult, op1=ALU.mult, accum_out=mean_r_xn[:, g : g + 1],
                )
                if i == 0 and not (TINY_G and k < 3):
                    nc.vector.tensor_reduce(out=sum_r[:, both], in_=sum_r_half[:, both, :], axis=mybir.AxisListType.X, op=ALU.add)
                if i == 0 and TINY_G and k < 3:
                    nc.gpsimd.tensor_tensor(out=sum_r[:, both], in0=sum_r_half[:, both, 0], in1=sum_r_half[:, both, 1], op=ALU.add)
                    nc.gpsimd.tensor_scalar(out=mean_r[:, both], in0=sum_r[:, both], scalar1=1.0 / COLS, scalar2=0.0, op0=ALU.mult, op1=ALU.add)
            if not (TINY_G and k < 3):
                nc.vector.tensor_scalar(out=mean_r[:, both], in0=sum_r[:, both], scalar1=1.0 / COLS, scalar2=None, op0=ALU.mult)

        def shift_on_gpsimd(g):
            nc.gpsimd.tensor_scalar(
                out=xn_to_shift[:, g, :], in0=xn_to_shift[:, g, :],
                scalar1=mean_r_xn[:, g : g + 1], scalar2=mean_r[:, g : g + 1], op0=ALU.mult, op1=ALU.add,
            )

        def shift_on_scalar(g, cols):
            nc.scalar.activation(
                out=xn_to_shift[:, g, cols], in_=xn_to_shift[:, g, cols], func=ACT.Identity,
                scale=mean_r_xn[:, g : g + 1], bias=mean_r[:, g : g + 1],
            )

        def regroup_x(s, n, on_scalar):
            copy = nc.scalar.copy if on_scalar else nc.vector.tensor_copy
            copy(
                out=grouped_in_runs(x_grouped[:, s, half_of(n), :]),
                in_=rows_in_runs(x_sb[:, s * PACK : (s + 1) * PACK, half_of(n)]),
            )

        def quantise_x(s):
            nc.vector.quantize_mx(
                out=x_codes[:, s, :].bitcast(E4M3_X4),
                scales=x_scales[:, s, :],
                in_=x_grouped[:, s, :, :].rearrange("p w j -> p (w j)"),
            )

        dv_grouped, acc = {}, {}

        def finish_dv(m, s):
            if (m, s) in dv_grouped:
                return
            groups = slice(s * PACK, (s + 1) * PACK)
            dv_grouped[m, s] = block.tile([P, M_TILE, PACK], BF16, name="dv_grouped", align_bytes=64)
            nc.vector.tensor_tensor(
                out=grouped_in_runs(dv_grouped[m, s][:]),
                in0=rows_in_runs(u_to_r[:, groups, cols_of(m)]),
                in1=rows_in_runs(xn_to_shift[:, groups, cols_of(m)]),
                op=ALU.subtract,
            )

        def finish_on_gpsimd(m):
            dv_grouped[m, 0] = early.tile([P, M_TILE, PACK], BF16, name="dv_early", align_bytes=64)
            nc.gpsimd.tensor_tensor(
                out=dv_grouped[m, 0][:],
                in0=u_to_r[:, 0:PACK, cols_of(m)].rearrange("p j w -> p w j"),
                in1=xn_to_shift[:, 0:PACK, cols_of(m)].rearrange("p j w -> p w j"),
                op=ALU.subtract,
            )

        def quantise_dv(m, s):
            nc.vector.quantize_mx(
                out=dv_codes[:, s, cols_of(m)].bitcast(E5M2_X4),
                scales=dv_scales[:, s, cols_of(m)],
                in_=dv_grouped[m, s][:].rearrange("p w j -> p (w j)"),
            )

        def multiply(m, s):
            for n in range(HALVES):
                if s == 0:
                    acc[m, n] = banks.tile([P, N_TILE], F32, name="bank")
                nc.tensor.matmul_mx(
                    out=acc[m, n][:],
                    lhsT=dv_codes[:, s, cols_of(m)].bitcast(E5M2_X4),
                    lhsT_scale=dv_scales[:, s, cols_of(m)],
                    rhs=x_codes[:, s, half_of(n)].bitcast(E4M3_X4),
                    rhs_scale=x_scales[:, s, half_of(n)],
                    start=(s == 0),
                    stop=(s == PASSES - 1),
                )

        def store(m):
            for n in range(HALVES):
                out_sb = result.tile([P, N_TILE], F32, name="out_sb")
                if m >= BLOCKS - LAST_SPLIT and n == 0:
                    nc.vector.tensor_copy(out=out_sb[:], in_=acc[m, n][:])
                else:
                    nc.scalar.copy(out=out_sb[:], in_=acc[m, n][:])
                if m == BLOCKS - 1 and n == 1 and LAST_ON_SCALAR:
                    nc.scalar.dma_start(out=out[cols_of(m), half_of(n)], in_=out_sb[:])
                else:
                    nc.sync.dma_start(out=out[cols_of(m), half_of(n)], in_=out_sb[:])

        ahead_blocks = min(AHEAD, 4)
        products = [(m, 0) for m in range(ahead_blocks)] + [(m, 1) for m in range(ahead_blocks)]
        products += [(m, s) for m in range(ahead_blocks, BLOCKS) for s in range(PASSES)]
        quantised = []

        def make_dv(units, may_multiply):
            finish_dv(units[0][0], units[0][1])
            for i, unit in enumerate(units):
                if i + 1 < len(units):
                    finish_dv(units[i + 1][0], units[i + 1][1])
                quantise_dv(unit[0], unit[1])
                quantised.append(unit)
                while may_multiply and products and products[0] in quantised:
                    m, s = products[0]
                    products.remove(products[0])
                    multiply(m, s)
                    if s == 1:
                        store(m)

        first_pass = [(m, 0) for m in range(BLOCKS)]

        def extra(tokens):
            for token in tokens:
                if token[0] == "rx":
                    regroup_x(token[1], token[2], token[3])
                elif token[0] == "qx":
                    quantise_x(token[1])
                elif token[0] == "b":
                    subtract_on_vector(token[1])
                elif token[0] == "sh":
                    shift_on_scalar(token[1], slice(0, COLS))
                elif token[0] == "gfin":
                    finish_on_gpsimd(token[1])
                elif token[0] == "fin":
                    finish_dv(token[1], 0)
                elif token[0] == "qdv":
                    quantise_dv(token[1], 0)
                    quantised.append((token[1], 0))
                    first_pass.remove((token[1], 0))
                elif token[0] == "units":
                    make_dv(first_pass[: token[1]], False)
                    for unit in first_pass[: token[1]]:
                        first_pass.remove(unit)

        for k in range(4):
            extra(plan.get((k, "A0"), ()))
            square(k)
            if k == 0:
                nc.scalar.copy(out=gamma_col[:], in_=gamma_ps[:, 0:BLOCKS])
                nc.scalar.mul(out=gamma_neg[:], in_=gamma_ps[:, 0:BLOCKS], mul=-1.0)
            with_grad = tuple(g for g in (2 * k, 2 * k + 1) if g not in THROUGH_SCALAR)
            grad_t = [turn(grad_sb, with_grad, blocks) for blocks in chunks(with_grad)] if with_grad else []
            ahead = pair(k + 1, THROUGH_SCALAR)
            h_t = [turn(h_sb, (g,), ALL_BLOCKS) for g in ahead]
            c_t = [turn(c_sb, (g,), ALL_BLOCKS) for g in ahead]
            for i in range(len(grad_t)):
                blocks = chunks(with_grad)[i]
                grad_gamma_t = scale(grad_t[i], with_grad, blocks, gamma_col)
                turn_back((grad_gamma_t,), with_grad, blocks, grad_gamma)
            extra(plan.get((k, "A1"), ()))
            for g in pair(k + 1, ON_TENSOR):
                subtract_on_tensor(g)
            for i, g in enumerate(ahead):
                h_gamma_t = scale(h_t[i], (g,), ALL_BLOCKS, gamma_col)
                c_gamma_t = scale(c_t[i], (g,), ALL_BLOCKS, gamma_neg)
                turn_back((h_gamma_t, c_gamma_t), (g,), ALL_BLOCKS, factor_ps)
            extra(plan.get((k, "A2"), ()))
            extra(plan.get((k, "a"), ()))
            order = sorted((2 * k, 2 * k + 1), key=lambda g: (g in THROUGH_SCALAR) != S_FIRST)
            for g in order:
                times_gate(g)
            extra(plan.get((k, "b"), ()))
            if len(with_grad) == 2:
                for n in range(HALVES):
                    for g in with_grad:
                        times_grad(g, (n,))
            else:
                for i, g in enumerate(sorted((2 * k, 2 * k + 1), key=lambda g: (g in THROUGH_SCALAR) != S_FIRST)):
                    if i == 1:
                        extra(plan.get((k, "b2"), ()))
                    times_grad(g, (0, 1))
            extra(plan.get((k, "c"), ()))
            means(k, order)
            for g in (2 * k, 2 * k + 1):
                if g in G_SHIFTS:
                    shift_on_gpsimd(g)
            extra(plan.get((k, "d"), ()))
        for cols in (slice(0, 256), slice(256, 512), slice(512, COLS)):
            shift_on_scalar(6, cols)
            shift_on_scalar(7, cols)
        fill = first_pass[:FILL]
        if fill:
            make_dv(fill, False)
        extra(plan.get((4, "a"), ()))
        make_dv([unit for unit in products if unit not in quantised], True)
